import numpy as np
import ml_dtypes


def mxq(x, axis, fmt="e4m3"):
    dtype, down = {"e4m3": (ml_dtypes.float8_e4m3fn, 7), "e5m2": (ml_dtypes.float8_e5m2, 14)}[fmt]
    v = np.moveaxis(np.asarray(x, np.float32).astype(ml_dtypes.bfloat16).astype(np.float64), axis, -1)
    blocks = v.reshape(v.shape[:-1] + (-1, 32))
    amax = np.abs(blocks).max(-1, keepdims=True)
    byte = np.maximum(np.where(amax > 0, np.frexp(amax)[1] - 1 + 127, 0) - down, 1)
    scale = np.exp2(byte - 127.0)
    codes = (blocks / scale).astype(np.float32).astype(dtype).astype(np.float64)
    return np.moveaxis((codes * scale).reshape(v.shape), -1, axis)


WIDE = False


def mx_kscale(k):
    if not WIDE:
        return np.ones(k)
    levels = np.array([10, -10, 5, -5, 0])
    a = np.random.permutation(np.resize(levels, k // 512 * 4)).reshape(k // 512, 4)
    idx = np.arange(k)
    return np.exp2(a[idx // 512, idx % 128 // 32])


BF16 = ml_dtypes.bfloat16


def bf(x):
    return np.asarray(x, np.float32).astype(BF16)


def f64(x):
    return np.asarray(x).astype(np.float64)


B, P, D, NL, T, E, G = 2, 192, 1024, 16, 2, 1, 2
WG = NL * NL * T * G
CLIP = 1.0
LOG_2PI = np.log(2.0 * np.pi)


def clip(v):
    return np.clip(v, -CLIP, CLIP)


def gaussian_multi(m1, v1, m2, v2):
    v1s = np.exp(2.0 * v1)
    v2s = np.exp(2.0 * v2)
    add = v1s + v2s
    log_add = np.log(add)
    scale = (-0.5 * (LOG_2PI + log_add + (m1 - m2) ** 2 / add)).sum(-1)
    mu = (m1 * v2s + m2 * v1s) / add
    var = v1 + v2 - 0.5 * log_add
    return scale, mu, var


def setup_inputs():
    s = mx_kscale(D)
    return {"x": bf(np.random.standard_normal((B, P, D)) * s),
            "s_weight": bf(np.random.standard_normal((B, P, NL, E))),
            "s_mu": bf(clip(np.random.standard_normal((B, P, NL, E, G)))),
            "s_var": bf(clip(np.random.standard_normal((B, P, NL, E, G)))),
            "tcm_w": bf(np.random.standard_normal((D, WG)) / np.sqrt(D) / s[:, None]),
            "tcm_b": bf(np.random.standard_normal(WG) * 0.3),
            "tcv_w": bf(np.random.standard_normal((D, WG)) / np.sqrt(D) / s[:, None]),
            "tcv_b": bf(np.random.standard_normal(WG) * 0.3)}


def reference(x, s_weight, s_mu, s_var, tcm_w, tcm_b, tcv_w, tcv_b):
    xq = mxq(f64(x).reshape(B * P, D), 1, "e4m3")
    t_c_mu = clip(((xq @ mxq(f64(tcm_w), 0, "e4m3")) + f64(tcm_b)).reshape(B, P, NL, NL, T, G))[:, :, :, :, :, None, :]
    t_c_var = clip(((xq @ mxq(f64(tcv_w), 0, "e4m3")) + f64(tcv_b)).reshape(B, P, NL, NL, T, G))[:, :, :, :, :, None, :]
    m1 = f64(s_mu)[:, :, None, :, None, :, :]
    v1 = f64(s_var)[:, :, None, :, None, :, :]
    cs_scale, cs_mu, cs_var = gaussian_multi(m1, v1, t_c_mu, t_c_var)
    cs_scale = cs_scale + f64(s_weight)[:, :, None, :, None, :]
    return cs_scale, cs_mu, cs_var

@@ -1,0 +1,394 @@
+import math
+from contextlib import ExitStack
+
+import concourse.mybir as mybir
+from concourse.masks import make_identity
+
+F32 = mybir.dt.float32
+BF16 = mybir.dt.bfloat16
+U32 = mybir.dt.uint32
+U8 = mybir.dt.uint8
+I32 = mybir.dt.int32
+FP8X4 = mybir.dt.float8_e4m3fn_x4
+ALU = mybir.AluOpType
+ACT = mybir.ActivationFunctionType
+
+P = 128
+MT = 3
+K = 1024
+KP = 2
+N = 1024
+NH = 512
+H = 2
+NI = 8
+FLOPS = 2 * 384 * 1024 * 2048
+MEAN = 0
+LSD = 1
+V_COLS = 336
+
+
+def tile_chainlveg_pa_kernel(
+    tc, x, s_weight, s_mu, s_var, tcm_w, tcm_b, tcv_w, tcv_b, out_0, out_1, out_2
+):
+    nc = tc.nc
+    with ExitStack() as ctx:
+        const = ctx.enter_context(tc.tile_pool(name="const", bufs=1))
+        work = ctx.enter_context(tc.tile_pool(name="work", bufs=2))
+        psum = ctx.enter_context(tc.psum_pool(name="psum", bufs=3))
+        ctx.enter_context(tc.manual_schedule())
+
+        x_rows = x.rearrange("b p d -> (b p) d").rearrange("(t q) d -> q t d", q=P)
+        sm_rows = s_mu.rearrange("b p j e g -> (b p) (j e g)").rearrange("(t q) c -> q t c", q=P)
+        sv_rows = s_var.rearrange("b p j e g -> (b p) (j e g)").rearrange("(t q) c -> q t c", q=P)
+        sw_rows = s_weight.rearrange("b p j e -> (b p) (j e)").rearrange("(t q) c -> q t c", q=P)
+        w_views = [w.rearrange("(c p j) n -> c p j n", c=KP, p=P, j=4) for w in (tcm_w, tcv_w)]
+        sc_rows = out_0.rearrange("b p i j t e -> (b p) (i j t e)").rearrange("(t q) c -> q t c", q=P)
+        mu_rows = out_1.rearrange("b p i j t e g -> (b p) (i j t e g)").rearrange("(t q) c -> q t c", q=P)
+        var_rows = out_2.rearrange("b p i j t e g -> (b p) (i j t e g)").rearrange("(t q) c -> q t c", q=P)
+
+        x_sb = const.tile([P, MT, K], BF16, name="x_sb")
+        sv = const.tile([P, MT, 32], BF16, name="sv")
+        sm = const.tile([P, MT, 32], BF16, name="sm")
+        sw = const.tile([P, MT, 16], BF16, name="sw")
+        brow = const.tile([P, 2 * N], BF16, name="brow")
+        ident = const.tile([P, P], F32, name="ident")
+        ones = const.tile([P, P], BF16, name="ones")
+        onecol = const.tile([P, 1], F32, name="onecol")
+        ie1s = const.tile([P, MT * 32], F32, name="ie1s")
+        v1e = const.tile([P, MT, 64], F32, name="v1e")
+        m1e = const.tile([P, MT, 64], F32, name="m1e")
+        m1p = const.tile([P, MT, 64], F32, name="m1p")
+        ie1e = const.tile([P, MT, 64], F32, name="ie1e")
+        vsum = const.tile([P, MT * 16], F32, name="vsum")
+        t0 = const.tile([P, MT * 16], F32, name="t0")
+        te = const.tile([P, MT, 32], F32, name="te")
+        xg = const.tile([P, MT, K], BF16, name="xg", align_bytes=64)
+        xq = const.tile([P, MT, 2 * P], U32, name="xq", align_bytes=64)
+        xs = const.tile([P, MT, 2 * P], U8, name="xs", align_bytes=64)
+        wq = const.tile([P, 8, NH], U32, name="wq", align_bytes=64)
+        ws = const.tile([P, 8, NH], U8, name="ws", align_bytes=64)
+        bb = const.tile([P, 2, N], F32, name="bb")
+        pieces = [(h, w, c) for h in range(H) for w in (LSD, MEAN) for c in range(KP)]
+        raw = {}
+        grouped = {}
+        for key in pieces:
+            raw[key] = const.tile([P, 4, NH], BF16, name="raw_%d_%d_%d" % key)
+            grouped[key] = const.tile([P, NH, 4], BF16, name="grp_%d_%d_%d" % key, align_bytes=64)
+
+        def load_x(mt):
+            nc.sync.dma_start(out=x_sb[:, mt, :], in_=x_rows[:, mt, :])
+
+        def load_w(key):
+            h, w, c = key
+            nc.sync.dma_start(out=raw[key][:], in_=w_views[w][c, :, :, h * NH : (h + 1) * NH])
+
+        def spread_t(ap):
+            return (
+                ap.rearrange("p (a g) -> p a g", g=2).unsqueeze(2).to_broadcast([P, MT * 16, 2, 2])
+            )
+
+        def as_jtg(a):
+            return a[:].rearrange("p m (j t g) -> p (m j) t g", j=16, t=2, g=2)
+
+        sm_flat = sm[:].rearrange("p m c -> p (m c)")
+        sv_flat = sv[:].rearrange("p m c -> p (m c)")
+
+        def table_v1():
+            nc.vector.tensor_copy(out=as_jtg(v1e), in_=spread_t(sv_flat))
+
+        def tables_m1():
+            nc.vector.tensor_scalar(
+                out=as_jtg(m1p), in0=spread_t(sm_flat), scalar1=1.0, scalar2=None, op0=ALU.add
+            )
+            nc.vector.tensor_copy(out=as_jtg(m1e), in_=spread_t(sm_flat))
+
+        def tables_rest():
+            sv_pairs = sv_flat.rearrange("p (a g) -> p a g", g=2)
+            nc.vector.tensor_tensor(
+                out=vsum[:], in0=sv_pairs[:, :, 0], in1=sv_pairs[:, :, 1], op=ALU.add
+            )
+            nc.vector.tensor_copy(out=as_jtg(ie1e), in_=spread_t(ie1s[:]))
+            nc.vector.scalar_tensor_tensor(
+                out=t0[:],
+                in0=sw[:].rearrange("p m c -> p (m c)"),
+                scalar=-math.log(2.0 * math.pi),
+                in1=vsum[:],
+                op0=ALU.add,
+                op1=ALU.subtract,
+            )
+            nc.vector.tensor_copy(
+                out=te[:].rearrange("p m (j t) -> p (m j) t", t=2),
+                in_=t0[:].unsqueeze(2).to_broadcast([P, MT * 16, 2]),
+            )
+
+        xw = x_sb[:].bitcast(F32)
+        xg32 = xg[:].bitcast(F32)
+
+        def x_turn(mt):
+            xt = psum.tile([P, 4, P], F32, name="xt%d" % mt, tag="xt", bufs=2)
+            for c in range(KP):
+                for u in range(2):
+                    nc.tensor.transpose(
+                        out=xt[:, 2 * c + u, :],
+                        in_=xw[:, mt, 256 * c + u : 256 * c + 256 : 2],
+                        identity=ident[:],
+                    )
+            nc.scalar.copy(
+                out=xg32[:, mt, :].rearrange("p (c r u) -> p c r u", c=KP, r=P, u=2),
+                in_=xt[:].rearrange("p (c u) r -> p c r u", c=KP, u=2),
+            )
+
+        def quantise_x(mt):
+            nc.vector.quantize_mx(
+                out=xq[:, mt, :].bitcast(FP8X4), scales=xs[:, mt, :], in_=xg[:, mt, :]
+            )
+
+        def regroup(copy, key, c0, c1):
+            copy(
+                out=grouped[key][:, c0:c1, :].rearrange("p (c i) t -> p c t i", i=4),
+                in_=raw[key][:, :, c0:c1].rearrange("p t (c i) -> p c t i", i=4),
+            )
+
+        def regroup_both(key):
+            regroup(nc.scalar.copy, key, V_COLS, NH)
+            regroup(nc.vector.tensor_copy, key, 0, V_COLS)
+
+        def regroup_scalar(key, part=None):
+            if part is None:
+                regroup(nc.scalar.copy, key, 0, NH)
+            else:
+                regroup(nc.scalar.copy, key, part * (NH // 2), (part + 1) * (NH // 2))
+
+        def quantise_w(key):
+            i = pieces.index(key)
+            nc.vector.quantize_mx(
+                out=wq[:, i, :].bitcast(FP8X4),
+                scales=ws[:, i, :],
+                in_=grouped[key][:].rearrange("p w j -> p (w j)"),
+            )
+
+        def spread_bias(h, w):
+            bp = psum.tile([P, NH], F32, name="bp_%d_%d" % (h, w), tag="xt", bufs=2)
+            nc.tensor.matmul(
+                out=bp[:], lhsT=ones[:], rhs=brow[:, w * N + h * NH : w * N + (h + 1) * NH],
+                start=True, stop=True,
+            )
+            nc.scalar.copy(out=bb[:, w, h * NH : (h + 1) * NH], in_=bp[:])
+
+        acc = {}
+
+        def matmuls(h, w):
+            for mt in range(MT):
+                a = psum.tile([P, NH], F32, name="acc_%d_%d_%d" % (h, mt, w), tag=("pm", "pv")[w])
+                for c in range(KP):
+                    i = pieces.index((h, w, c))
+                    nc.tensor.matmul_mx(
+                        out=a[:],
+                        lhsT=xq[:, mt, c * P : (c + 1) * P].bitcast(FP8X4),
+                        lhsT_scale=xs[:, mt, c * P : (c + 1) * P],
+                        rhs=wq[:, i, :].bitcast(FP8X4),
+                        rhs_scale=ws[:, i, :],
+                        start=(c == 0),
+                        stop=(c == KP - 1),
+                    )
+                acc[(h, mt, w)] = a
+
+        t = {}
+
+        def new(kind, h, cols=NH):
+            a = work.tile([P, MT, cols], F32, name="%s_%d" % (kind, h), tag=kind)
+            t[(kind, h)] = a
+            return a
+
+        def all_i(tab, cols):
+            return tab[:].unsqueeze(2).to_broadcast([P, MT, NI, cols])
+
+        def one_i(tab, mt, cols):
+            return tab[:, mt, :].unsqueeze(1).to_broadcast([P, NI, cols])
+
+        def by_i(a):
+            return a[:].rearrange("p m (i c) -> p m i c", i=NI)
+
+        def by_i1(a, mt):
+            return a[:, mt, :].rearrange("p (i c) -> p i c", i=NI)
+
+        def flat(a):
+            return a[:].rearrange("p m c -> p (m c)")
+
+        def evict(h, w, kind):
+            a = new(kind, h)
+            for mt in range(MT):
+                nc.vector.tensor_tensor(
+                    out=a[:, mt, :], in0=acc[(h, mt, w)][:], in1=bb[:, w, h * NH : (h + 1) * NH],
+                    op=ALU.add,
+                )
+
+        def clip_v(h):
+            nc.vector.tensor_scalar(
+                out=flat(t[("v", h)]), in0=flat(t[("v", h)]), scalar1=1.0, scalar2=-1.0,
+                op0=ALU.min, op1=ALU.max,
+            )
+
+        def diff_v(h):
+            nc.vector.tensor_tensor(
+                out=by_i(new("rho", h)), in0=by_i(t[("v", h)]), in1=all_i(v1e, 64), op=ALU.subtract
+            )
+
+        def sigmoid(h):
+            nc.scalar.activation(
+                out=flat(t[("rho", h)]), in_=flat(t[("rho", h)]), func=ACT.Sigmoid, scale=-2.0
+            )
+
+        def relu_m(h):
+            for mt in range(MT):
+                nc.scalar.activation(
+                    out=t[("m", h)][:, mt, :], in_=t[("m", h)][:, mt, :], func=ACT.Relu,
+                    bias=onecol[:, 0:1], scale=1.0,
+                )
+
+        def diff_m(h):
+            a = new("d", h)
+            for mt in range(MT):
+                nc.vector.scalar_tensor_tensor(
+                    out=by_i1(a, mt), in0=by_i1(t[("m", h)], mt), scalar=2.0,
+                    in1=one_i(m1p, mt, 64), op0=ALU.min, op1=ALU.subtract,
+                )
+
+        def log_rho(h):
+            nc.scalar.activation(out=flat(new("lr", h)), in_=flat(t[("rho", h)]), func=ACT.Ln)
+
+        def cols(h, width):
+            return slice(h * width, (h + 1) * width)
+
+        def prod_a(h):
+            nc.vector.tensor_tensor(
+                out=flat(new("a", h)), in0=flat(t[("d", h)]), in1=flat(t[("rho", h)]), op=ALU.mult
+            )
+
+        def prod_q1(h):
+            nc.vector.tensor_tensor(
+                out=flat(new("q", h)), in0=flat(t[("a", h)]), in1=flat(t[("d", h)]), op=ALU.mult
+            )
+
+        def mean_out(h):
+            nc.vector.tensor_tensor(
+                out=by_i(t[("a", h)]), in0=by_i(t[("a", h)]), in1=all_i(m1e, 64), op=ALU.add
+            )
+            nc.sync.dma_start(out=mu_rows[:, :, cols(h, NH)], in_=t[("a", h)][:])
+
+        def prod_q2(h):
+            nc.vector.tensor_tensor(
+                out=by_i(t[("q", h)]), in0=by_i(t[("q", h)]), in1=all_i(ie1e, 64), op=ALU.mult
+            )
+
+        def sum_z(h):
+            nc.vector.tensor_tensor(
+                out=flat(t[("q", h)]), in0=flat(t[("q", h)]), in1=flat(t[("lr", h)]), op=ALU.subtract
+            )
+
+        def var_out(h):
+            nc.vector.scalar_tensor_tensor(
+                out=flat(t[("lr", h)]), in0=flat(t[("lr", h)]), scalar=0.5,
+                in1=flat(t[("v", h)]), op0=ALU.mult, op1=ALU.add,
+            )
+            nc.sync.dma_start(out=var_rows[:, :, cols(h, NH)], in_=t[("lr", h)][:])
+
+        def pair_sum(h):
+            pairs = t[("q", h)][:].rearrange("p m (c g) -> p (m c) g", g=2)
+            nc.vector.tensor_tensor(
+                out=flat(new("zs", h, NH // 2)), in0=pairs[:, :, 0], in1=pairs[:, :, 1], op=ALU.add
+            )
+
+        def scale_out(h):
+            a = new("sc", h, NH // 2)
+            for mt in range(MT):
+                nc.vector.scalar_tensor_tensor(
+                    out=by_i1(a, mt), in0=by_i1(t[("zs", h)], mt), scalar=-0.5,
+                    in1=one_i(te, mt, 32), op0=ALU.mult, op1=ALU.add,
+                )
+            nc.sync.dma_start(out=sc_rows[:, :, cols(h, NH // 2)], in_=a[:])
+
+        nc.scalar.dma_start(out=sv[:], in_=sv_rows)
+        nc.scalar.dma_start(out=sm[:], in_=sm_rows)
+        nc.scalar.dma_start(out=sw[:], in_=sw_rows)
+        load_x(0)
+        load_w(pieces[0])
+        load_w(pieces[1])
+        load_x(1)
+        load_x(2)
+        nc.vector.memset(brow[:].bitcast(I32), 0)
+        nc.scalar.dma_start(out=brow[0:1, 0:N], in_=tcm_b.unsqueeze(0))
+        nc.scalar.dma_start(out=brow[0:1, N : 2 * N], in_=tcv_b.unsqueeze(0))
+        for key in pieces[2:]:
+            load_w(key)
+        make_identity(nc, ident[:])
+        nc.gpsimd.memset(ones[:], 1.0)
+        nc.gpsimd.memset(onecol[:], 1.0)
+        nc.scalar.activation(out=ie1s[:], in_=sv_flat, func=ACT.Exp, scale=-2.0)
+
+        x_turn(0)
+        table_v1()
+        quantise_x(0)
+        regroup_both((0, LSD, 0))
+        regroup_both((0, LSD, 1))
+        quantise_w((0, LSD, 0))
+        x_turn(1)
+        x_turn(2)
+        spread_bias(0, LSD)
+        quantise_w((0, LSD, 1))
+        quantise_x(1)
+        quantise_x(2)
+        matmuls(0, LSD)
+        regroup_scalar((0, MEAN, 0))
+        regroup_scalar((0, MEAN, 1))
+        spread_bias(0, MEAN)
+        tables_m1()
+        evict(0, LSD, "v")
+        quantise_w((0, MEAN, 0))
+        clip_v(0)
+        diff_v(0)
+        sigmoid(0)
+        quantise_w((0, MEAN, 1))
+        matmuls(0, MEAN)
+        tables_rest()
+        evict(0, MEAN, "m")
+        relu_m(0)
+        diff_m(0)
+        log_rho(0)
+        regroup_scalar((1, LSD, 0))
+        regroup_scalar((1, LSD, 1))
+        spread_bias(1, LSD)
+        spread_bias(1, MEAN)
+        regroup_scalar((1, MEAN, 0))
+        regroup_scalar((1, MEAN, 1))
+        prod_a(0)
+        prod_q1(0)
+        mean_out(0)
+        prod_q2(0)
+        quantise_w((1, LSD, 0))
+        quantise_w((1, LSD, 1))
+        matmuls(1, LSD)
+        sum_z(0)
+        var_out(0)
+        quantise_w((1, MEAN, 0))
+        pair_sum(0)
+        quantise_w((1, MEAN, 1))
+        matmuls(1, MEAN)
+        scale_out(0)
+
+        evict(1, LSD, "v")
+        evict(1, MEAN, "m")
+        relu_m(1)
+        clip_v(1)
+        diff_v(1)
+        sigmoid(1)
+        diff_m(1)
+        log_rho(1)
+        prod_a(1)
+        prod_q1(1)
+        mean_out(1)
+        prod_q2(1)
+        sum_z(1)
+        var_out(1)
+        pair_sum(1)
+        scale_out(1)

@@ -54,6 +54,9 @@ def tile_chainlveg_pa_kernel(
         ident = const.tile([P, P], F32, name="ident")
         ones = const.tile([P, P], BF16, name="ones")
         onecol = const.tile([P, 1], F32, name="onecol")
+        neghalf = const.tile([P, P], F32, name="neghalf")
+        te_rows = const.tile([P, MT, P], F32, name="te_rows")
+        te_cols = const.tile([P, MT, P], F32, name="te_cols")
         ie1s = const.tile([P, MT * 32], F32, name="ie1s")
         v1e = const.tile([P, MT, 64], F32, name="v1e")
         m1e = const.tile([P, MT, 64], F32, name="m1e")
@@ -61,7 +64,6 @@ def tile_chainlveg_pa_kernel(
         ie1e = const.tile([P, MT, 64], F32, name="ie1e")
         vsum = const.tile([P, MT * 16], F32, name="vsum")
         t0 = const.tile([P, MT * 16], F32, name="t0")
-        te = const.tile([P, MT, 32], F32, name="te")
         xg = const.tile([P, MT, K], BF16, name="xg", align_bytes=64)
         xq = const.tile([P, MT, 2 * P], U32, name="xq", align_bytes=64)
         xs = const.tile([P, MT, 2 * P], U8, name="xs", align_bytes=64)
@@ -117,9 +119,20 @@ def tile_chainlveg_pa_kernel(
                 op1=ALU.subtract,
             )
             nc.vector.tensor_copy(
-                out=te[:].rearrange("p m (j t) -> p (m j) t", t=2),
-                in_=t0[:].unsqueeze(2).to_broadcast([P, MT * 16, 2]),
+                out=te_rows[:, :, 0:32].rearrange("p m (j t) -> p m j t", t=2),
+                in_=t0[:].rearrange("p (m j) -> p m j", m=MT).unsqueeze(3).to_broadcast([P, MT, 16, 2]),
             )
+
+        def table_neghalf():
+            nc.vector.tensor_scalar(
+                out=neghalf[:], in0=ident[:], scalar1=-0.5, scalar2=None, op0=ALU.mult
+            )
+
+        def te_turn():
+            tp = psum.tile([P, MT, P], F32, name="tp", tag="xt", bufs=2)
+            for mt in range(MT):
+                nc.tensor.transpose(out=tp[:, mt, :], in_=te_rows[:, mt, :], identity=ident[:])
+            nc.scalar.copy(out=te_cols[:], in_=tp[:])
 
         xw = x_sb[:].bitcast(F32)
         xg32 = xg[:].bitcast(F32)
@@ -215,13 +228,13 @@ def tile_chainlveg_pa_kernel(
         def flat(a):
             return a[:].rearrange("p m c -> p (m c)")
 
-        def evict(h, w, kind):
-            a = new(kind, h)
-            for mt in range(MT):
-                nc.vector.tensor_tensor(
-                    out=a[:, mt, :], in0=acc[(h, mt, w)][:], in1=bb[:, w, h * NH : (h + 1) * NH],
-                    op=ALU.add,
-                )
+        def evict(h, w, kind, mt):
+            if mt == 0:
+                new(kind, h)
+            nc.vector.tensor_tensor(
+                out=t[(kind, h)][:, mt, :], in0=acc[(h, mt, w)][:],
+                in1=bb[:, w, h * NH : (h + 1) * NH], op=ALU.add,
+            )
 
         def clip_v(h):
             nc.vector.tensor_scalar(
@@ -234,17 +247,17 @@ def tile_chainlveg_pa_kernel(
                 out=by_i(new("rho", h)), in0=by_i(t[("v", h)]), in1=all_i(v1e, 64), op=ALU.subtract
             )
 
-        def sigmoid(h):
+        def sigmoid(h, scale):
             nc.scalar.activation(
-                out=flat(t[("rho", h)]), in_=flat(t[("rho", h)]), func=ACT.Sigmoid, scale=-2.0
+                out=flat(t[("rho", h)]), in_=flat(t[("rho", h)]), func=ACT.Sigmoid, scale=scale
             )
 
-        def relu_m(h):
-            for mt in range(MT):
-                nc.scalar.activation(
-                    out=t[("m", h)][:, mt, :], in_=t[("m", h)][:, mt, :], func=ACT.Relu,
-                    bias=onecol[:, 0:1], scale=1.0,
-                )
+
+        def relu_m(h, mt):
+            nc.scalar.activation(
+                out=t[("m", h)][:, mt, :], in_=t[("m", h)][:, mt, :], func=ACT.Relu,
+                bias=onecol[:, 0:1], scale=1.0,
+            )
 
         def diff_m(h):
             a = new("d", h)
@@ -254,8 +267,10 @@ def tile_chainlveg_pa_kernel(
                     in1=one_i(m1p, mt, 64), op0=ALU.min, op1=ALU.subtract,
                 )
 
-        def log_rho(h):
-            nc.scalar.activation(out=flat(new("lr", h)), in_=flat(t[("rho", h)]), func=ACT.Ln)
+        def log_rho(h, scale):
+            nc.scalar.activation(
+                out=flat(new("lr", h)), in_=flat(t[("rho", h)]), func=ACT.Ln, scale=scale
+            )
 
         def cols(h, width):
             return slice(h * width, (h + 1) * width)
@@ -282,113 +297,165 @@ def tile_chainlveg_pa_kernel(
             )
 
         def sum_z(h):
+            t[("z", h)] = work.tile([P, MT, 2, NH // 2], F32, name="z_%d" % h, tag="d")
             nc.vector.tensor_tensor(
-                out=flat(t[("q", h)]), in0=flat(t[("q", h)]), in1=flat(t[("lr", h)]), op=ALU.subtract
+                out=t[("z", h)][:].rearrange("p m g c -> p m c g"),
+                in0=t[("q", h)][:].rearrange("p m (c g) -> p m c g", g=2),
+                in1=t[("lr", h)][:].rearrange("p m (c g) -> p m c g", g=2),
+                op=ALU.subtract,
             )
 
-        def var_out(h):
-            nc.vector.scalar_tensor_tensor(
-                out=flat(t[("lr", h)]), in0=flat(t[("lr", h)]), scalar=0.5,
-                in1=flat(t[("v", h)]), op0=ALU.mult, op1=ALU.add,
-            )
-            nc.sync.dma_start(out=var_rows[:, :, cols(h, NH)], in_=t[("lr", h)][:])
+        def var_out(h, op1, split):
+            if split:
+                for mt in range(MT):
+                    nc.vector.scalar_tensor_tensor(
+                        out=t[("lr", h)][:, mt, :], in0=t[("lr", h)][:, mt, :], scalar=0.5,
+                        in1=t[("v", h)][:, mt, :], op0=ALU.mult, op1=op1,
+                    )
+                    nc.sync.dma_start(out=var_rows[:, mt, cols(h, NH)], in_=t[("lr", h)][:, mt, :])
+            else:
+                nc.vector.scalar_tensor_tensor(
+                    out=flat(t[("lr", h)]), in0=flat(t[("lr", h)]), scalar=0.5,
+                    in1=flat(t[("v", h)]), op0=ALU.mult, op1=op1,
+                )
+                nc.sync.dma_start(out=var_rows[:, :, cols(h, NH)], in_=t[("lr", h)][:])
 
-        def pair_sum(h):
-            pairs = t[("q", h)][:].rearrange("p m (c g) -> p (m c) g", g=2)
+        zps = {}
+
+        def pair_sum_tensor(h):
+            zps[0] = psum.tile([P, 2, NH // 2], F32, name="zpa_%d" % h, tag="xt", bufs=2)
+            zps[1] = psum.tile([P, 1, NH // 2], F32, name="zpb_%d" % h, tag="xt", bufs=2)
+            for mt in range(MT):
+                zp = zps[mt // 2][:, mt % 2, :]
+                nc.tensor.matmul(
+                    out=zp.rearrange("p (i c) -> p i c", i=NI),
+                    lhsT=te_cols[:, mt, :],
+                    rhs=ident[:, 0:32].unsqueeze(1).to_broadcast([P, NI, 32]),
+                    start=True, stop=False,
+                )
+                nc.tensor.matmul(
+                    out=zp, lhsT=neghalf[:], rhs=t[("z", h)][:, mt, 0, :], start=False, stop=False
+                )
+                nc.tensor.matmul(
+                    out=zp, lhsT=neghalf[:], rhs=t[("z", h)][:, mt, 1, :], start=False, stop=True
+                )
+
+        def scale_out_scalar(h):
+            a = new("sc", h, NH // 2)
+            nc.scalar.copy(out=a[:, 0:2, :], in_=zps[0][:])
+            nc.scalar.copy(out=a[:, 2:3, :], in_=zps[1][:])
+            nc.sync.dma_start(out=sc_rows[:, :, cols(h, NH // 2)], in_=a[:])
+
+        def pair_sum_vector(h):
             nc.vector.tensor_tensor(
-                out=flat(new("zs", h, NH // 2)), in0=pairs[:, :, 0], in1=pairs[:, :, 1], op=ALU.add
+                out=new("zs", h, NH // 2)[:], in0=t[("z", h)][:, :, 0, :], in1=t[("z", h)][:, :, 1, :],
+                op=ALU.add,
             )
 
-        def scale_out(h):
+        def scale_out_vector(h, shift):
             a = new("sc", h, NH // 2)
             for mt in range(MT):
                 nc.vector.scalar_tensor_tensor(
                     out=by_i1(a, mt), in0=by_i1(t[("zs", h)], mt), scalar=-0.5,
-                    in1=one_i(te, mt, 32), op0=ALU.mult, op1=ALU.add,
+                    in1=te_rows[:, mt, shift : shift + 32].unsqueeze(1).to_broadcast([P, NI, 32]),
+                    op0=ALU.mult, op1=ALU.add,
                 )
-            nc.sync.dma_start(out=sc_rows[:, :, cols(h, NH // 2)], in_=a[:])
+                nc.sync.dma_start(out=sc_rows[:, mt, cols(h, NH // 2)], in_=a[:, mt, :])
 
+        V0, V1, M0, M1 = (0, LSD, 0), (0, LSD, 1), (0, MEAN, 0), (0, MEAN, 1)
+        W0, W1, W2, W3 = (1, LSD, 0), (1, LSD, 1), (1, MEAN, 0), (1, MEAN, 1)
         nc.scalar.dma_start(out=sv[:], in_=sv_rows)
         nc.scalar.dma_start(out=sm[:], in_=sm_rows)
         nc.scalar.dma_start(out=sw[:], in_=sw_rows)
+        load_w(V0)
         load_x(0)
-        load_w(pieces[0])
-        load_w(pieces[1])
+        load_w(V1)
         load_x(1)
         load_x(2)
         nc.vector.memset(brow[:].bitcast(I32), 0)
         nc.scalar.dma_start(out=brow[0:1, 0:N], in_=tcm_b.unsqueeze(0))
         nc.scalar.dma_start(out=brow[0:1, N : 2 * N], in_=tcv_b.unsqueeze(0))
-        for key in pieces[2:]:
+        for key in (W0, W1, M0, M1, W2, W3):
             load_w(key)
         make_identity(nc, ident[:])
         nc.gpsimd.memset(ones[:], 1.0)
         nc.gpsimd.memset(onecol[:], 1.0)
+        nc.gpsimd.memset(te_rows[:], 0.0)
         nc.scalar.activation(out=ie1s[:], in_=sv_flat, func=ACT.Exp, scale=-2.0)
 
-        x_turn(0)
         table_v1()
+        regroup_both(V0)
+        x_turn(0)
+        tables_m1()
+        tables_rest()
+        table_neghalf()
         quantise_x(0)
-        regroup_both((0, LSD, 0))
-        regroup_both((0, LSD, 1))
-        quantise_w((0, LSD, 0))
+        regroup_both(V1)
+        quantise_w(V0)
+        spread_bias(0, LSD)
         x_turn(1)
         x_turn(2)
-        spread_bias(0, LSD)
-        quantise_w((0, LSD, 1))
+        quantise_w(V1)
         quantise_x(1)
         quantise_x(2)
         matmuls(0, LSD)
-        regroup_scalar((0, MEAN, 0))
-        regroup_scalar((0, MEAN, 1))
-        spread_bias(0, MEAN)
-        tables_m1()
-        evict(0, LSD, "v")
-        quantise_w((0, MEAN, 0))
-        clip_v(0)
-        diff_v(0)
-        sigmoid(0)
-        quantise_w((0, MEAN, 1))
-        matmuls(0, MEAN)
-        tables_rest()
-        evict(0, MEAN, "m")
-        relu_m(0)
-        diff_m(0)
-        log_rho(0)
-        regroup_scalar((1, LSD, 0))
-        regroup_scalar((1, LSD, 1))
+        regroup_scalar(W0)
+        regroup_scalar(W1)
         spread_bias(1, LSD)
+        regroup_scalar(M0)
+        regroup_scalar(M1)
+        spread_bias(0, MEAN)
+        evict(0, LSD, "v", 0)
+        evict(0, LSD, "v", 1)
+        quantise_w(W0)
+        evict(0, LSD, "v", 2)
+        clip_v(0)
+        quantise_w(W1)
+        matmuls(1, LSD)
+        diff_v(0)
+        sigmoid(0, -2.0)
+        evict(1, LSD, "v", 0)
+        quantise_w(M0)
+        evict(1, LSD, "v", 1)
+        evict(1, LSD, "v", 2)
+        clip_v(1)
+        quantise_w(M1)
+        matmuls(0, MEAN)
+        diff_v(1)
+        evict(0, MEAN, "m", 0)
+        relu_m(0, 0)
+        evict(0, MEAN, "m", 1)
+        relu_m(0, 1)
+        evict(0, MEAN, "m", 2)
+        relu_m(0, 2)
+        sigmoid(1, -2.0)
+        diff_m(0)
+        regroup_scalar(W2)
+        regroup_scalar(W3)
+        log_rho(0, 1.0)
+        log_rho(1, 1.0)
         spread_bias(1, MEAN)
-        regroup_scalar((1, MEAN, 0))
-        regroup_scalar((1, MEAN, 1))
+        te_turn()
         prod_a(0)
         prod_q1(0)
+        quantise_w(W2)
         mean_out(0)
-        prod_q2(0)
-        quantise_w((1, LSD, 0))
-        quantise_w((1, LSD, 1))
-        matmuls(1, LSD)
-        sum_z(0)
-        var_out(0)
-        quantise_w((1, MEAN, 0))
-        pair_sum(0)
-        quantise_w((1, MEAN, 1))
+        quantise_w(W3)
         matmuls(1, MEAN)
-        scale_out(0)
-
-        evict(1, LSD, "v")
-        evict(1, MEAN, "m")
-        relu_m(1)
-        clip_v(1)
-        diff_v(1)
-        sigmoid(1)
+        prod_q2(0)
+        sum_z(0)
+        pair_sum_tensor(0)
+        var_out(0, ALU.add, False)
+        for mt in range(MT):
+            evict(1, MEAN, "m", mt)
+            relu_m(1, mt)
         diff_m(1)
-        log_rho(1)
+        scale_out_scalar(0)
         prod_a(1)
         prod_q1(1)
         mean_out(1)
         prod_q2(1)
         sum_z(1)
-        var_out(1)
-        pair_sum(1)
-        scale_out(1)
+        var_out(1, ALU.add, False)
+        pair_sum_vector(1)
+        scale_out_vector(1, 0)

@@ -34,7 +34,7 @@ def tile_chainlveg_pa_kernel(
     with ExitStack() as ctx:
         const = ctx.enter_context(tc.tile_pool(name="const", bufs=1))
         work = ctx.enter_context(tc.tile_pool(name="work", bufs=2))
-        psum = ctx.enter_context(tc.psum_pool(name="psum", bufs=3))
+        psum = ctx.enter_context(tc.psum_pool(name="psum", bufs=8))
         ctx.enter_context(tc.manual_schedule())
 
         x_rows = x.rearrange("b p d -> (b p) d").rearrange("(t q) d -> q t d", q=P)
@@ -50,10 +50,12 @@ def tile_chainlveg_pa_kernel(
         sv = const.tile([P, MT, 32], BF16, name="sv")
         sm = const.tile([P, MT, 32], BF16, name="sm")
         sw = const.tile([P, MT, 16], BF16, name="sw")
-        brow = const.tile([P, 2 * N], BF16, name="brow")
+        btile = const.tile([P, P], BF16, name="btile")
+        bcols = const.tile([P, 16], BF16, name="bcols")
+        identb = const.tile([P, P], BF16, name="identb")
         ident = const.tile([P, P], F32, name="ident")
-        ones = const.tile([P, P], BF16, name="ones")
         onecol = const.tile([P, 1], F32, name="onecol")
+        dummy = const.tile([P, 1], F32, name="dummy")
         neghalf = const.tile([P, P], F32, name="neghalf")
         te_rows = const.tile([P, MT, P], F32, name="te_rows")
         te_cols = const.tile([P, MT, P], F32, name="te_cols")
@@ -65,11 +67,12 @@ def tile_chainlveg_pa_kernel(
         vsum = const.tile([P, MT * 16], F32, name="vsum")
         t0 = const.tile([P, MT * 16], F32, name="t0")
         xg = const.tile([P, MT, K], BF16, name="xg", align_bytes=64)
-        xq = const.tile([P, MT, 2 * P], U32, name="xq", align_bytes=64)
-        xs = const.tile([P, MT, 2 * P], U8, name="xs", align_bytes=64)
+        xq = const.tile([P, KP, MT * P], U32, name="xq", align_bytes=64)
+        xs = const.tile([P, KP, MT * P], U8, name="xs", align_bytes=64)
+        bm1 = const.tile([P, 8], F32, name="bm1")
         wq = const.tile([P, 8, NH], U32, name="wq", align_bytes=64)
         ws = const.tile([P, 8, NH], U8, name="ws", align_bytes=64)
-        bb = const.tile([P, 2, N], F32, name="bb")
+        bb = const.tile([P, N], BF16, name="bb")
         pieces = [(h, w, c) for h in range(H) for w in (LSD, MEAN) for c in range(KP)]
         raw = {}
         grouped = {}
@@ -129,7 +132,7 @@ def tile_chainlveg_pa_kernel(
             )
 
         def te_turn():
-            tp = psum.tile([P, MT, P], F32, name="tp", tag="xt", bufs=2)
+            tp = psum.tile([P, MT, P], F32, name="tp", tag="bank")
             for mt in range(MT):
                 nc.tensor.transpose(out=tp[:, mt, :], in_=te_rows[:, mt, :], identity=ident[:])
             nc.scalar.copy(out=te_cols[:], in_=tp[:])
@@ -138,7 +141,7 @@ def tile_chainlveg_pa_kernel(
         xg32 = xg[:].bitcast(F32)
 
         def x_turn(mt):
-            xt = psum.tile([P, 4, P], F32, name="xt%d" % mt, tag="xt", bufs=2)
+            xt = psum.tile([P, 4, P], F32, name="xt%d" % mt, tag="bank")
             for c in range(KP):
                 for u in range(2):
                     nc.tensor.transpose(
@@ -152,9 +155,12 @@ def tile_chainlveg_pa_kernel(
             )
 
         def quantise_x(mt):
-            nc.vector.quantize_mx(
-                out=xq[:, mt, :].bitcast(FP8X4), scales=xs[:, mt, :], in_=xg[:, mt, :]
-            )
+            for c in range(KP):
+                nc.vector.quantize_mx(
+                    out=xq[:, c, mt * P : (mt + 1) * P].bitcast(FP8X4),
+                    scales=xs[:, c, mt * P : (mt + 1) * P],
+                    in_=xg[:, mt, c * 512 : (c + 1) * 512],
+                )
 
         def regroup(copy, key, c0, c1):
             copy(
@@ -165,6 +171,9 @@ def tile_chainlveg_pa_kernel(
         def regroup_both(key):
             regroup(nc.scalar.copy, key, V_COLS, NH)
             regroup(nc.vector.tensor_copy, key, 0, V_COLS)
+
+        def regroup_vector(key):
+            regroup(nc.vector.tensor_copy, key, 0, NH)
 
         def regroup_scalar(key, part=None):
             if part is None:
@@ -180,25 +189,34 @@ def tile_chainlveg_pa_kernel(
                 in_=grouped[key][:].rearrange("p w j -> p (w j)"),
             )
 
-        def spread_bias(h, w):
-            bp = psum.tile([P, NH], F32, name="bp_%d_%d" % (h, w), tag="xt", bufs=2)
-            nc.tensor.matmul(
-                out=bp[:], lhsT=ones[:], rhs=brow[:, w * N + h * NH : w * N + (h + 1) * NH],
-                start=True, stop=True,
+        def bias_turn():
+            btp = psum.tile([P, P], BF16, name="btp", tag="bank")
+            nc.tensor.transpose(out=btp[:], in_=btile[:], identity=identb[:])
+            nc.vector.tensor_copy(out=bcols[:], in_=btp[:, 0:16])
+            nc.vector.tensor_scalar(
+                out=bm1[:], in0=btp[:, 0:8], scalar1=1.0, scalar2=None, op0=ALU.add
             )
-            nc.scalar.copy(out=bb[:, w, h * NH : (h + 1) * NH], in_=bp[:])
+
+        def spread_bias():
+            bp = psum.tile([P, 8, P], BF16, name="bp", tag="bank")
+            for b in range(8):
+                nc.tensor.transpose(
+                    out=bp[:, b, :], in_=bcols[:, 8 + b : 9 + b].to_broadcast([P, P]),
+                    identity=identb[:],
+                )
+            nc.scalar.copy(out=bb[:], in_=bp[:].rearrange("p b c -> p (b c)"))
 
         acc = {}
 
-        def matmuls(h, w):
-            for mt in range(MT):
-                a = psum.tile([P, NH], F32, name="acc_%d_%d_%d" % (h, mt, w), tag=("pm", "pv")[w])
+        def matmuls(h, w, only=None):
+            for mt in range(MT) if only is None else (only,):
+                a = psum.tile([P, NH], F32, name="acc_%d_%d_%d" % (h, mt, w), tag="bank")
                 for c in range(KP):
                     i = pieces.index((h, w, c))
                     nc.tensor.matmul_mx(
                         out=a[:],
-                        lhsT=xq[:, mt, c * P : (c + 1) * P].bitcast(FP8X4),
-                        lhsT_scale=xs[:, mt, c * P : (c + 1) * P],
+                        lhsT=xq[:, c, mt * P : (mt + 1) * P].bitcast(FP8X4),
+                        lhsT_scale=xs[:, c, mt * P : (mt + 1) * P],
                         rhs=wq[:, i, :].bitcast(FP8X4),
                         rhs_scale=ws[:, i, :],
                         start=(c == 0),
@@ -207,6 +225,48 @@ def tile_chainlveg_pa_kernel(
                 acc[(h, mt, w)] = a
 
         t = {}
+        arow = {}
+
+        def mean_products(h, nt):
+            if nt == 0:
+                t[("m", h)] = work.tile([P, 4, MT * P], F32, name="m_%d" % h, tag="m")
+            at = psum.tile([P, MT * P], F32, name="at_%d_%d" % (h, nt), tag="bank")
+            for r0, r1 in ((0, 2 * P), (2 * P, 3 * P)):
+                for c in range(KP):
+                    i = pieces.index((h, MEAN, c))
+                    nc.tensor.matmul_mx(
+                        out=at[:, r0:r1],
+                        lhsT=wq[:, i, nt * P : (nt + 1) * P].bitcast(FP8X4),
+                        lhsT_scale=ws[:, i, nt * P : (nt + 1) * P],
+                        rhs=xq[:, c, r0:r1].bitcast(FP8X4),
+                        rhs_scale=xs[:, c, r0:r1],
+                        start=(c == 0),
+                        stop=(c == KP - 1),
+                    )
+            nc.scalar.activation(
+                out=t[("m", h)][:, nt, :], in_=at[:], func=ACT.Relu,
+                bias=bm1[:, h * 4 + nt : h * 4 + nt + 1], scale=1.0,
+            )
+
+        def mean_turn(h, nt):
+            for mt in range(MT):
+                if nt == 0:
+                    arow[(h, mt)] = psum.tile([P, NH], F32, name="arow_%d_%d" % (h, mt), tag="bank")
+                nc.tensor.transpose(
+                    out=arow[(h, mt)][:, nt * P : (nt + 1) * P],
+                    in_=t[("m", h)][:, nt, mt * P : (mt + 1) * P],
+                    identity=ident[:],
+                )
+
+        def mean_front(h):
+            mean_products(h, 0)
+            mean_products(h, 1)
+            mean_turn(h, 0)
+            mean_turn(h, 1)
+            mean_products(h, 2)
+            mean_products(h, 3)
+            mean_turn(h, 2)
+            mean_turn(h, 3)
 
         def new(kind, h, cols=NH):
             a = work.tile([P, MT, cols], F32, name="%s_%d" % (kind, h), tag=kind)
@@ -233,7 +293,7 @@ def tile_chainlveg_pa_kernel(
                 new(kind, h)
             nc.vector.tensor_tensor(
                 out=t[(kind, h)][:, mt, :], in0=acc[(h, mt, w)][:],
-                in1=bb[:, w, h * NH : (h + 1) * NH], op=ALU.add,
+                in1=bb[:, h * NH : (h + 1) * NH], op=ALU.add,
             )
 
         def clip_v(h):
@@ -247,23 +307,20 @@ def tile_chainlveg_pa_kernel(
                 out=by_i(new("rho", h)), in0=by_i(t[("v", h)]), in1=all_i(v1e, 64), op=ALU.subtract
             )
 
+        def load_sigmoid_table():
+            nc.scalar.activation(out=dummy[:], in_=onecol[:], func=ACT.Sigmoid)
+
         def sigmoid(h, scale):
             nc.scalar.activation(
                 out=flat(t[("rho", h)]), in_=flat(t[("rho", h)]), func=ACT.Sigmoid, scale=scale
             )
 
 
-        def relu_m(h, mt):
-            nc.scalar.activation(
-                out=t[("m", h)][:, mt, :], in_=t[("m", h)][:, mt, :], func=ACT.Relu,
-                bias=onecol[:, 0:1], scale=1.0,
-            )
-
         def diff_m(h):
             a = new("d", h)
             for mt in range(MT):
                 nc.vector.scalar_tensor_tensor(
-                    out=by_i1(a, mt), in0=by_i1(t[("m", h)], mt), scalar=2.0,
+                    out=by_i1(a, mt), in0=arow[(h, mt)][:].rearrange("p (i c) -> p i c", i=NI), scalar=2.0,
                     in1=one_i(m1p, mt, 64), op0=ALU.min, op1=ALU.subtract,
                 )
 
@@ -285,66 +342,83 @@ def tile_chainlveg_pa_kernel(
                 out=flat(new("q", h)), in0=flat(t[("a", h)]), in1=flat(t[("d", h)]), op=ALU.mult
             )
 
-        def mean_out(h):
-            nc.vector.tensor_tensor(
-                out=by_i(t[("a", h)]), in0=by_i(t[("a", h)]), in1=all_i(m1e, 64), op=ALU.add
-            )
-            nc.sync.dma_start(out=mu_rows[:, :, cols(h, NH)], in_=t[("a", h)][:])
+        def mean_out(h, mt=None):
+            if mt is None:
+                nc.vector.tensor_tensor(
+                    out=by_i(t[("a", h)]), in0=by_i(t[("a", h)]), in1=all_i(m1e, 64), op=ALU.add
+                )
+                nc.sync.dma_start(out=mu_rows[:, :, cols(h, NH)], in_=t[("a", h)][:])
+            else:
+                nc.vector.tensor_tensor(
+                    out=by_i1(t[("a", h)], mt), in0=by_i1(t[("a", h)], mt), in1=one_i(m1e, mt, 64),
+                    op=ALU.add,
+                )
+                nc.sync.dma_start(out=mu_rows[:, mt, cols(h, NH)], in_=t[("a", h)][:, mt, :])
 
         def prod_q2(h):
             nc.vector.tensor_tensor(
                 out=by_i(t[("q", h)]), in0=by_i(t[("q", h)]), in1=all_i(ie1e, 64), op=ALU.mult
             )
 
-        def sum_z(h):
-            t[("z", h)] = work.tile([P, MT, 2, NH // 2], F32, name="z_%d" % h, tag="d")
-            nc.vector.tensor_tensor(
-                out=t[("z", h)][:].rearrange("p m g c -> p m c g"),
-                in0=t[("q", h)][:].rearrange("p m (c g) -> p m c g", g=2),
-                in1=t[("lr", h)][:].rearrange("p m (c g) -> p m c g", g=2),
-                op=ALU.subtract,
-            )
+        def sum_z(h, mt=None):
+            if mt is None or mt == 0:
+                t[("z", h)] = work.tile([P, MT, 2, NH // 2], F32, name="z_%d" % h, tag="d")
+            if mt is None:
+                nc.vector.tensor_tensor(
+                    out=t[("z", h)][:].rearrange("p m g c -> p m c g"),
+                    in0=t[("q", h)][:].rearrange("p m (c g) -> p m c g", g=2),
+                    in1=t[("lr", h)][:].rearrange("p m (c g) -> p m c g", g=2),
+                    op=ALU.subtract,
+                )
+            else:
+                nc.vector.tensor_tensor(
+                    out=t[("z", h)][:, mt, :, :].rearrange("p g c -> p c g"),
+                    in0=t[("q", h)][:, mt, :].rearrange("p (c g) -> p c g", g=2),
+                    in1=t[("lr", h)][:, mt, :].rearrange("p (c g) -> p c g", g=2),
+                    op=ALU.subtract,
+                )
 
-        def var_out(h, op1, split):
-            if split:
-                for mt in range(MT):
-                    nc.vector.scalar_tensor_tensor(
-                        out=t[("lr", h)][:, mt, :], in0=t[("lr", h)][:, mt, :], scalar=0.5,
-                        in1=t[("v", h)][:, mt, :], op0=ALU.mult, op1=op1,
-                    )
-                    nc.sync.dma_start(out=var_rows[:, mt, cols(h, NH)], in_=t[("lr", h)][:, mt, :])
+        def var_out(h, mt=None):
+            if mt is None:
+                nc.vector.scalar_tensor_tensor(
+                    out=flat(t[("v", h)]), in0=flat(t[("lr", h)]), scalar=0.5,
+                    in1=flat(t[("v", h)]), op0=ALU.mult, op1=ALU.add,
+                )
+                nc.sync.dma_start(out=var_rows[:, :, cols(h, NH)], in_=t[("v", h)][:])
             else:
                 nc.vector.scalar_tensor_tensor(
-                    out=flat(t[("lr", h)]), in0=flat(t[("lr", h)]), scalar=0.5,
-                    in1=flat(t[("v", h)]), op0=ALU.mult, op1=op1,
+                    out=t[("v", h)][:, mt, :], in0=t[("lr", h)][:, mt, :], scalar=0.5,
+                    in1=t[("v", h)][:, mt, :], op0=ALU.mult, op1=ALU.add,
                 )
-                nc.sync.dma_start(out=var_rows[:, :, cols(h, NH)], in_=t[("lr", h)][:])
+                nc.sync.dma_start(out=var_rows[:, mt, cols(h, NH)], in_=t[("v", h)][:, mt, :])
 
         zps = {}
 
-        def pair_sum_tensor(h):
-            zps[0] = psum.tile([P, 2, NH // 2], F32, name="zpa_%d" % h, tag="xt", bufs=2)
-            zps[1] = psum.tile([P, 1, NH // 2], F32, name="zpb_%d" % h, tag="xt", bufs=2)
+        def pair_sum_open(h):
             for mt in range(MT):
-                zp = zps[mt // 2][:, mt % 2, :]
+                zps[(h, mt)] = psum.tile([P, NH // 2], F32, name="zp_%d_%d" % (h, mt), tag="bank")
                 nc.tensor.matmul(
-                    out=zp.rearrange("p (i c) -> p i c", i=NI),
+                    out=zps[(h, mt)][:].rearrange("p (i c) -> p i c", i=NI),
                     lhsT=te_cols[:, mt, :],
                     rhs=ident[:, 0:32].unsqueeze(1).to_broadcast([P, NI, 32]),
                     start=True, stop=False,
                 )
-                nc.tensor.matmul(
-                    out=zp, lhsT=neghalf[:], rhs=t[("z", h)][:, mt, 0, :], start=False, stop=False
-                )
-                nc.tensor.matmul(
-                    out=zp, lhsT=neghalf[:], rhs=t[("z", h)][:, mt, 1, :], start=False, stop=True
-                )
 
-        def scale_out_scalar(h):
-            a = new("sc", h, NH // 2)
-            nc.scalar.copy(out=a[:, 0:2, :], in_=zps[0][:])
-            nc.scalar.copy(out=a[:, 2:3, :], in_=zps[1][:])
-            nc.sync.dma_start(out=sc_rows[:, :, cols(h, NH // 2)], in_=a[:])
+        def pair_sum_close(h, mt):
+            nc.tensor.matmul(
+                out=zps[(h, mt)][:], lhsT=neghalf[:], rhs=t[("z", h)][:, mt, 0, :],
+                start=False, stop=False,
+            )
+            nc.tensor.matmul(
+                out=zps[(h, mt)][:], lhsT=neghalf[:], rhs=t[("z", h)][:, mt, 1, :],
+                start=False, stop=True,
+            )
+
+        def scale_out_scalar(h, mt):
+            if mt == 0:
+                new("sc", h, NH // 2)
+            nc.scalar.copy(out=t[("sc", h)][:, mt, :], in_=zps[(h, mt)][:])
+            nc.scalar.dma_start(out=sc_rows[:, mt, cols(h, NH // 2)], in_=t[("sc", h)][:, mt, :])
 
         def pair_sum_vector(h):
             nc.vector.tensor_tensor(
@@ -364,6 +438,9 @@ def tile_chainlveg_pa_kernel(
 
         V0, V1, M0, M1 = (0, LSD, 0), (0, LSD, 1), (0, MEAN, 0), (0, MEAN, 1)
         W0, W1, W2, W3 = (1, LSD, 0), (1, LSD, 1), (1, MEAN, 0), (1, MEAN, 1)
+        nc.gpsimd.memset(btile[:], 0.0)
+        nc.scalar.dma_start(out=btile[0:8, :], in_=tcm_b.rearrange("(r c) -> r c", c=P))
+        nc.scalar.dma_start(out=btile[8:16, :], in_=tcv_b.rearrange("(r c) -> r c", c=P))
         nc.scalar.dma_start(out=sv[:], in_=sv_rows)
         nc.scalar.dma_start(out=sm[:], in_=sm_rows)
         nc.scalar.dma_start(out=sw[:], in_=sw_rows)
@@ -372,13 +449,10 @@ def tile_chainlveg_pa_kernel(
         load_w(V1)
         load_x(1)
         load_x(2)
-        nc.vector.memset(brow[:].bitcast(I32), 0)
-        nc.scalar.dma_start(out=brow[0:1, 0:N], in_=tcm_b.unsqueeze(0))
-        nc.scalar.dma_start(out=brow[0:1, N : 2 * N], in_=tcv_b.unsqueeze(0))
-        for key in (W0, W1, M0, M1, W2, W3):
+        for key in (W0, M0, W1, M1, W2, W3):
             load_w(key)
+        make_identity(nc, identb[:])
         make_identity(nc, ident[:])
-        nc.gpsimd.memset(ones[:], 1.0)
         nc.gpsimd.memset(onecol[:], 1.0)
         nc.gpsimd.memset(te_rows[:], 0.0)
         nc.scalar.activation(out=ie1s[:], in_=sv_flat, func=ACT.Exp, scale=-2.0)
@@ -387,12 +461,11 @@ def tile_chainlveg_pa_kernel(
         regroup_both(V0)
         x_turn(0)
         tables_m1()
-        tables_rest()
-        table_neghalf()
+        bias_turn()
         quantise_x(0)
         regroup_both(V1)
+        spread_bias()
         quantise_w(V0)
-        spread_bias(0, LSD)
         x_turn(1)
         x_turn(2)
         quantise_w(V1)
@@ -401,61 +474,65 @@ def tile_chainlveg_pa_kernel(
         matmuls(0, LSD)
         regroup_scalar(W0)
         regroup_scalar(W1)
-        spread_bias(1, LSD)
-        regroup_scalar(M0)
-        regroup_scalar(M1)
-        spread_bias(0, MEAN)
+        regroup_scalar(W2)
+        load_sigmoid_table()
         evict(0, LSD, "v", 0)
+        regroup_vector(M0)
         evict(0, LSD, "v", 1)
-        quantise_w(W0)
         evict(0, LSD, "v", 2)
-        clip_v(0)
+        regroup_vector(M1)
+        quantise_w(W0)
         quantise_w(W1)
         matmuls(1, LSD)
-        diff_v(0)
-        sigmoid(0, -2.0)
-        evict(1, LSD, "v", 0)
         quantise_w(M0)
+        quantise_w(M1)
+        for nt in range(4):
+            mean_products(0, nt)
+        clip_v(0)
+        diff_v(0)
+        evict(1, LSD, "v", 0)
         evict(1, LSD, "v", 1)
         evict(1, LSD, "v", 2)
+        for nt in range(4):
+            mean_turn(0, nt)
         clip_v(1)
-        quantise_w(M1)
-        matmuls(0, MEAN)
         diff_v(1)
-        evict(0, MEAN, "m", 0)
-        relu_m(0, 0)
-        evict(0, MEAN, "m", 1)
-        relu_m(0, 1)
-        evict(0, MEAN, "m", 2)
-        relu_m(0, 2)
+        sigmoid(0, -2.0)
         sigmoid(1, -2.0)
-        diff_m(0)
-        regroup_scalar(W2)
         regroup_scalar(W3)
+        tables_rest()
+        table_neghalf()
+        diff_m(0)
+        quantise_w(W2)
         log_rho(0, 1.0)
         log_rho(1, 1.0)
-        spread_bias(1, MEAN)
         te_turn()
         prod_a(0)
-        prod_q1(0)
-        quantise_w(W2)
-        mean_out(0)
         quantise_w(W3)
-        matmuls(1, MEAN)
+        for nt in range(4):
+            mean_products(1, nt)
+        for nt in range(4):
+            mean_turn(1, nt)
+        prod_q1(0)
+        mean_out(0)
+        pair_sum_open(0)
         prod_q2(0)
         sum_z(0)
-        pair_sum_tensor(0)
-        var_out(0, ALU.add, False)
         for mt in range(MT):
-            evict(1, MEAN, "m", mt)
-            relu_m(1, mt)
+            pair_sum_close(0, mt)
+        var_out(0)
         diff_m(1)
-        scale_out_scalar(0)
+        for mt in range(MT):
+            scale_out_scalar(0, mt)
+        pair_sum_open(1)
         prod_a(1)
         prod_q1(1)
-        mean_out(1)
         prod_q2(1)
-        sum_z(1)
-        var_out(1, ALU.add, False)
-        pair_sum_vector(1)
-        scale_out_vector(1, 0)
+        for mt in range(MT):
+            sum_z(1, mt)
+            pair_sum_close(1, mt)
+        for mt in range(MT):
+            mean_out(1, mt)
+            var_out(1, mt)
+        for mt in range(MT):
+            scale_out_scalar(1, mt)

@@ -62,7 +62,10 @@ def tile_chainlveg_pa_kernel(
         ie1s = const.tile([P, MT * 32], F32, name="ie1s")
         v1e = const.tile([P, MT, 64], F32, name="v1e")
         m1e = const.tile([P, MT, 64], F32, name="m1e")
-        m1p = const.tile([P, MT, 64], F32, name="m1p")
+        m1m = const.tile([P, MT, 64], F32, name="m1m")
+        m1m_rows = const.tile([P, MT, P], F32, name="m1m_rows")
+        m1m_cols = const.tile([P, MT * P], F32, name="m1m_cols")
+        twocol = const.tile([P, 1], F32, name="twocol")
         ie1e = const.tile([P, MT, 64], F32, name="ie1e")
         vsum = const.tile([P, MT * 16], F32, name="vsum")
         t0 = const.tile([P, MT * 16], F32, name="t0")
@@ -103,9 +106,23 @@ def tile_chainlveg_pa_kernel(
 
         def tables_m1():
             nc.vector.tensor_scalar(
-                out=as_jtg(m1p), in0=spread_t(sm_flat), scalar1=1.0, scalar2=None, op0=ALU.add
+                out=as_jtg(m1m), in0=spread_t(sm_flat), scalar1=-1.0, scalar2=None, op0=ALU.add
             )
+            nc.vector.tensor_copy(
+                out=m1m_rows[:].rearrange("p m (a c) -> p m a c", a=2),
+                in_=m1m[:].unsqueeze(2).to_broadcast([P, MT, 2, 64]),
+            )
+
+        def table_m1e():
             nc.vector.tensor_copy(out=as_jtg(m1e), in_=spread_t(sm_flat))
+
+        def m1m_turn():
+            tp = psum.tile([P, MT * P], F32, name="tp_m1m", tag="bank")
+            for mt in range(MT):
+                nc.tensor.transpose(
+                    out=tp[:, mt * P : (mt + 1) * P], in_=m1m_rows[:, mt, :], identity=ident[:]
+                )
+            nc.scalar.copy(out=m1m_cols[:], in_=tp[:])
 
         def tables_rest():
             sv_pairs = sv_flat.rearrange("p (a g) -> p a g", g=2)
@@ -247,15 +264,24 @@ def tile_chainlveg_pa_kernel(
                 out=t[("m", h)][:, nt, :], in_=at[:], func=ACT.Relu,
                 bias=bm1[:, h * 4 + nt : h * 4 + nt + 1], scale=1.0,
             )
+            nc.scalar.activation(
+                out=t[("m", h)][:, nt, :], in_=t[("m", h)][:, nt, :], func=ACT.Relu,
+                bias=twocol[:, 0:1], scale=-1.0,
+            )
 
         def mean_turn(h, nt):
             for mt in range(MT):
                 if nt == 0:
                     arow[(h, mt)] = psum.tile([P, NH], F32, name="arow_%d_%d" % (h, mt), tag="bank")
-                nc.tensor.transpose(
+                nc.tensor.matmul(
                     out=arow[(h, mt)][:, nt * P : (nt + 1) * P],
-                    in_=t[("m", h)][:, nt, mt * P : (mt + 1) * P],
-                    identity=ident[:],
+                    lhsT=t[("m", h)][:, nt, mt * P : (mt + 1) * P],
+                    rhs=ident[:], is_transpose=True, start=True, stop=False,
+                )
+                nc.tensor.matmul(
+                    out=arow[(h, mt)][:, nt * P : (nt + 1) * P],
+                    lhsT=m1m_cols[:, mt * P : (mt + 1) * P],
+                    rhs=ident[:], is_transpose=True, start=False, stop=True,
                 )
 
         def mean_front(h):
@@ -316,14 +342,6 @@ def tile_chainlveg_pa_kernel(
             )
 
 
-        def diff_m(h):
-            a = new("d", h)
-            for mt in range(MT):
-                nc.vector.scalar_tensor_tensor(
-                    out=by_i1(a, mt), in0=arow[(h, mt)][:].rearrange("p (i c) -> p i c", i=NI), scalar=2.0,
-                    in1=one_i(m1p, mt, 64), op0=ALU.min, op1=ALU.subtract,
-                )
-
         def log_rho(h, scale):
             nc.scalar.activation(
                 out=flat(new("lr", h)), in_=flat(t[("rho", h)]), func=ACT.Ln, scale=scale
@@ -333,25 +351,31 @@ def tile_chainlveg_pa_kernel(
             return slice(h * width, (h + 1) * width)
 
         def prod_a(h):
-            nc.vector.tensor_tensor(
-                out=flat(new("a", h)), in0=flat(t[("d", h)]), in1=flat(t[("rho", h)]), op=ALU.mult
-            )
+            new("a", h)
+            for mt in range(MT):
+                nc.vector.tensor_tensor(
+                    out=t[("a", h)][:, mt, :], in0=arow[(h, mt)][:], in1=t[("rho", h)][:, mt, :],
+                    op=ALU.mult,
+                )
 
         def prod_q1(h):
-            nc.vector.tensor_tensor(
-                out=flat(new("q", h)), in0=flat(t[("a", h)]), in1=flat(t[("d", h)]), op=ALU.mult
-            )
+            new("q", h)
+            for mt in range(MT):
+                nc.vector.tensor_tensor(
+                    out=t[("q", h)][:, mt, :], in0=arow[(h, mt)][:], in1=t[("a", h)][:, mt, :],
+                    op=ALU.mult,
+                )
 
         def mean_out(h, mt=None):
             if mt is None:
                 nc.vector.tensor_tensor(
-                    out=by_i(t[("a", h)]), in0=by_i(t[("a", h)]), in1=all_i(m1e, 64), op=ALU.add
+                    out=by_i(t[("a", h)]), in0=all_i(m1e, 64), in1=by_i(t[("a", h)]), op=ALU.subtract
                 )
                 nc.sync.dma_start(out=mu_rows[:, :, cols(h, NH)], in_=t[("a", h)][:])
             else:
                 nc.vector.tensor_tensor(
-                    out=by_i1(t[("a", h)], mt), in0=by_i1(t[("a", h)], mt), in1=one_i(m1e, mt, 64),
-                    op=ALU.add,
+                    out=by_i1(t[("a", h)], mt), in0=one_i(m1e, mt, 64), in1=by_i1(t[("a", h)], mt),
+                    op=ALU.subtract,
                 )
                 nc.sync.dma_start(out=mu_rows[:, mt, cols(h, NH)], in_=t[("a", h)][:, mt, :])
 
@@ -438,12 +462,12 @@ def tile_chainlveg_pa_kernel(
 
         V0, V1, M0, M1 = (0, LSD, 0), (0, LSD, 1), (0, MEAN, 0), (0, MEAN, 1)
         W0, W1, W2, W3 = (1, LSD, 0), (1, LSD, 1), (1, MEAN, 0), (1, MEAN, 1)
-        nc.gpsimd.memset(btile[:], 0.0)
-        nc.scalar.dma_start(out=btile[0:8, :], in_=tcm_b.rearrange("(r c) -> r c", c=P))
-        nc.scalar.dma_start(out=btile[8:16, :], in_=tcv_b.rearrange("(r c) -> r c", c=P))
         nc.scalar.dma_start(out=sv[:], in_=sv_rows)
         nc.scalar.dma_start(out=sm[:], in_=sm_rows)
         nc.scalar.dma_start(out=sw[:], in_=sw_rows)
+        nc.gpsimd.memset(btile[:], 0.0)
+        nc.scalar.dma_start(out=btile[0:8, :], in_=tcm_b.rearrange("(r c) -> r c", c=P))
+        nc.scalar.dma_start(out=btile[8:16, :], in_=tcv_b.rearrange("(r c) -> r c", c=P))
         load_w(V0)
         load_x(0)
         load_w(V1)
@@ -454,6 +478,7 @@ def tile_chainlveg_pa_kernel(
         make_identity(nc, identb[:])
         make_identity(nc, ident[:])
         nc.gpsimd.memset(onecol[:], 1.0)
+        nc.gpsimd.memset(twocol[:], 2.0)
         nc.gpsimd.memset(te_rows[:], 0.0)
         nc.scalar.activation(out=ie1s[:], in_=sv_flat, func=ACT.Exp, scale=-2.0)
 
@@ -474,6 +499,7 @@ def tile_chainlveg_pa_kernel(
         matmuls(0, LSD)
         regroup_scalar(W0)
         regroup_scalar(W1)
+        m1m_turn()
         regroup_scalar(W2)
         load_sigmoid_table()
         evict(0, LSD, "v", 0)
@@ -486,10 +512,12 @@ def tile_chainlveg_pa_kernel(
         matmuls(1, LSD)
         quantise_w(M0)
         quantise_w(M1)
-        for nt in range(4):
-            mean_products(0, nt)
         clip_v(0)
         diff_v(0)
+        sigmoid(0, -2.0)
+        for nt in range(4):
+            mean_products(0, nt)
+        regroup_vector(W3)
         evict(1, LSD, "v", 0)
         evict(1, LSD, "v", 1)
         evict(1, LSD, "v", 2)
@@ -497,36 +525,33 @@ def tile_chainlveg_pa_kernel(
             mean_turn(0, nt)
         clip_v(1)
         diff_v(1)
-        sigmoid(0, -2.0)
         sigmoid(1, -2.0)
-        regroup_scalar(W3)
+        quantise_w(W2)
+        quantise_w(W3)
+        table_m1e()
         tables_rest()
         table_neghalf()
-        diff_m(0)
-        quantise_w(W2)
         log_rho(0, 1.0)
-        log_rho(1, 1.0)
         te_turn()
-        prod_a(0)
-        quantise_w(W3)
         for nt in range(4):
             mean_products(1, nt)
+        log_rho(1, 1.0)
+        prod_a(0)
+        prod_q1(0)
         for nt in range(4):
             mean_turn(1, nt)
-        prod_q1(0)
+        prod_q2(0)
         mean_out(0)
         pair_sum_open(0)
-        prod_q2(0)
         sum_z(0)
         for mt in range(MT):
             pair_sum_close(0, mt)
         var_out(0)
-        diff_m(1)
+        prod_a(1)
+        prod_q1(1)
         for mt in range(MT):
             scale_out_scalar(0, mt)
         pair_sum_open(1)
-        prod_a(1)
-        prod_q1(1)
         prod_q2(1)
         for mt in range(MT):
             sum_z(1, mt)

@@ -379,10 +379,16 @@ def tile_chainlveg_pa_kernel(
                 )
                 nc.sync.dma_start(out=mu_rows[:, mt, cols(h, NH)], in_=t[("a", h)][:, mt, :])
 
-        def prod_q2(h):
-            nc.vector.tensor_tensor(
-                out=by_i(t[("q", h)]), in0=by_i(t[("q", h)]), in1=all_i(ie1e, 64), op=ALU.mult
-            )
+        def prod_q2(h, mt=None):
+            if mt is None:
+                nc.vector.tensor_tensor(
+                    out=by_i(t[("q", h)]), in0=by_i(t[("q", h)]), in1=all_i(ie1e, 64), op=ALU.mult
+                )
+            else:
+                nc.vector.tensor_tensor(
+                    out=by_i1(t[("q", h)], mt), in0=by_i1(t[("q", h)], mt), in1=one_i(ie1e, mt, 64),
+                    op=ALU.mult,
+                )
 
         def sum_z(h, mt=None):
             if mt is None or mt == 0:
@@ -511,8 +517,8 @@ def tile_chainlveg_pa_kernel(
         quantise_w(W1)
         matmuls(1, LSD)
         quantise_w(M0)
-        quantise_w(M1)
         clip_v(0)
+        quantise_w(M1)
         diff_v(0)
         sigmoid(0, -2.0)
         for nt in range(4):
@@ -523,11 +529,11 @@ def tile_chainlveg_pa_kernel(
         evict(1, LSD, "v", 2)
         for nt in range(4):
             mean_turn(0, nt)
+        quantise_w(W2)
         clip_v(1)
+        quantise_w(W3)
         diff_v(1)
         sigmoid(1, -2.0)
-        quantise_w(W2)
-        quantise_w(W3)
         table_m1e()
         tables_rest()
         table_neghalf()
@@ -540,19 +546,20 @@ def tile_chainlveg_pa_kernel(
         prod_q1(0)
         for nt in range(4):
             mean_turn(1, nt)
-        prod_q2(0)
         mean_out(0)
+        prod_q2(0)
+        var_out(0)
         pair_sum_open(0)
         sum_z(0)
         for mt in range(MT):
             pair_sum_close(0, mt)
-        var_out(0)
         prod_a(1)
         prod_q1(1)
         for mt in range(MT):
             scale_out_scalar(0, mt)
         pair_sum_open(1)
-        prod_q2(1)
+        for mt in range(MT):
+            prod_q2(1, mt)
         for mt in range(MT):
             sum_z(1, mt)
             pair_sum_close(1, mt)

@@ -264,10 +264,22 @@ def tile_chainlveg_pa_kernel(
                 out=t[("m", h)][:, nt, :], in_=at[:], func=ACT.Relu,
                 bias=bm1[:, h * 4 + nt : h * 4 + nt + 1], scale=1.0,
             )
+
+        def mean_upper(h, nt):
             nc.scalar.activation(
                 out=t[("m", h)][:, nt, :], in_=t[("m", h)][:, nt, :], func=ACT.Relu,
                 bias=twocol[:, 0:1], scale=-1.0,
             )
+
+        def mean_clipped(h):
+            mean_products(h, 0)
+            mean_products(h, 1)
+            mean_upper(h, 0)
+            mean_products(h, 2)
+            mean_upper(h, 1)
+            mean_products(h, 3)
+            mean_upper(h, 2)
+            mean_upper(h, 3)
 
         def mean_turn(h, nt):
             for mt in range(MT):
@@ -278,6 +290,7 @@ def tile_chainlveg_pa_kernel(
                     lhsT=t[("m", h)][:, nt, mt * P : (mt + 1) * P],
                     rhs=ident[:], is_transpose=True, start=True, stop=False,
                 )
+            for mt in range(MT):
                 nc.tensor.matmul(
                     out=arow[(h, mt)][:, nt * P : (nt + 1) * P],
                     lhsT=m1m_cols[:, mt * P : (mt + 1) * P],
@@ -521,8 +534,7 @@ def tile_chainlveg_pa_kernel(
         quantise_w(M1)
         diff_v(0)
         sigmoid(0, -2.0)
-        for nt in range(4):
-            mean_products(0, nt)
+        mean_clipped(0)
         regroup_vector(W3)
         evict(1, LSD, "v", 0)
         evict(1, LSD, "v", 1)
@@ -539,8 +551,7 @@ def tile_chainlveg_pa_kernel(
         table_neghalf()
         log_rho(0, 1.0)
         te_turn()
-        for nt in range(4):
-            mean_products(1, nt)
+        mean_clipped(1)
         log_rho(1, 1.0)
         prod_a(0)
         prod_q1(0)

@@ -484,6 +484,7 @@ def tile_chainlveg_pa_kernel(
         nc.scalar.dma_start(out=sv[:], in_=sv_rows)
         nc.scalar.dma_start(out=sm[:], in_=sm_rows)
         nc.scalar.dma_start(out=sw[:], in_=sw_rows)
+        nc.gpsimd.memset(onecol[:], 1.0)
         nc.gpsimd.memset(btile[:], 0.0)
         nc.scalar.dma_start(out=btile[0:8, :], in_=tcm_b.rearrange("(r c) -> r c", c=P))
         nc.scalar.dma_start(out=btile[8:16, :], in_=tcv_b.rearrange("(r c) -> r c", c=P))
@@ -496,13 +497,13 @@ def tile_chainlveg_pa_kernel(
             load_w(key)
         make_identity(nc, identb[:])
         make_identity(nc, ident[:])
-        nc.gpsimd.memset(onecol[:], 1.0)
         nc.gpsimd.memset(twocol[:], 2.0)
         nc.gpsimd.memset(te_rows[:], 0.0)
-        nc.scalar.activation(out=ie1s[:], in_=sv_flat, func=ACT.Exp, scale=-2.0)
+        nc.scalar.activation(out=dummy[:], in_=onecol[:], func=ACT.Exp)
 
-        table_v1()
         regroup_both(V0)
+        nc.scalar.activation(out=ie1s[:], in_=sv_flat, func=ACT.Exp, scale=-2.0)
+        table_v1()
         x_turn(0)
         tables_m1()
         bias_turn()

@@ -104,10 +104,12 @@ def tile_chainlveg_pa_kernel(
         def table_v1():
             nc.vector.tensor_copy(out=as_jtg(v1e), in_=spread_t(sv_flat))
 
-        def tables_m1():
+        def table_m1m():
             nc.vector.tensor_scalar(
                 out=as_jtg(m1m), in0=spread_t(sm_flat), scalar1=-1.0, scalar2=None, op0=ALU.add
             )
+
+        def table_m1m_rows():
             nc.vector.tensor_copy(
                 out=m1m_rows[:].rearrange("p m (a c) -> p m a c", a=2),
                 in_=m1m[:].unsqueeze(2).to_broadcast([P, MT, 2, 64]),
@@ -138,6 +140,8 @@ def tile_chainlveg_pa_kernel(
                 op0=ALU.add,
                 op1=ALU.subtract,
             )
+
+        def table_te_rows():
             nc.vector.tensor_copy(
                 out=te_rows[:, :, 0:32].rearrange("p m (j t) -> p m j t", t=2),
                 in_=t0[:].rearrange("p (m j) -> p m j", m=MT).unsqueeze(3).to_broadcast([P, MT, 16, 2]),
@@ -461,7 +465,8 @@ def tile_chainlveg_pa_kernel(
             if mt == 0:
                 new("sc", h, NH // 2)
             nc.scalar.copy(out=t[("sc", h)][:, mt, :], in_=zps[(h, mt)][:])
-            nc.scalar.dma_start(out=sc_rows[:, mt, cols(h, NH // 2)], in_=t[("sc", h)][:, mt, :])
+            queue = (nc.scalar, nc.sync)[h]
+            queue.dma_start(out=sc_rows[:, mt, cols(h, NH // 2)], in_=t[("sc", h)][:, mt, :])
 
         def pair_sum_vector(h):
             nc.vector.tensor_tensor(
@@ -484,7 +489,6 @@ def tile_chainlveg_pa_kernel(
         nc.scalar.dma_start(out=sv[:], in_=sv_rows)
         nc.scalar.dma_start(out=sm[:], in_=sm_rows)
         nc.scalar.dma_start(out=sw[:], in_=sw_rows)
-        nc.gpsimd.memset(onecol[:], 1.0)
         nc.gpsimd.memset(btile[:], 0.0)
         nc.scalar.dma_start(out=btile[0:8, :], in_=tcm_b.rearrange("(r c) -> r c", c=P))
         nc.scalar.dma_start(out=btile[8:16, :], in_=tcv_b.rearrange("(r c) -> r c", c=P))
@@ -497,16 +501,17 @@ def tile_chainlveg_pa_kernel(
             load_w(key)
         make_identity(nc, identb[:])
         make_identity(nc, ident[:])
+        nc.gpsimd.memset(onecol[:], 1.0)
         nc.gpsimd.memset(twocol[:], 2.0)
         nc.gpsimd.memset(te_rows[:], 0.0)
-        nc.scalar.activation(out=dummy[:], in_=onecol[:], func=ACT.Exp)
-
-        regroup_both(V0)
         nc.scalar.activation(out=ie1s[:], in_=sv_flat, func=ACT.Exp, scale=-2.0)
+
         table_v1()
+        regroup_both(V0)
         x_turn(0)
-        tables_m1()
+        table_m1m()
         bias_turn()
+        table_m1m_rows()
         quantise_x(0)
         regroup_both(V1)
         spread_bias()
@@ -550,6 +555,7 @@ def tile_chainlveg_pa_kernel(
         table_m1e()
         tables_rest()
         table_neghalf()
+        table_te_rows()
         log_rho(0, 1.0)
         te_turn()
         mean_clipped(1)

@@ -510,15 +510,15 @@ def tile_chainlveg_pa_kernel(
         regroup_both(V0)
         x_turn(0)
         table_m1m()
-        bias_turn()
         table_m1m_rows()
-        quantise_x(0)
         regroup_both(V1)
-        spread_bias()
-        quantise_w(V0)
         x_turn(1)
+        quantise_x(0)
         x_turn(2)
+        quantise_w(V0)
+        bias_turn()
         quantise_w(V1)
+        spread_bias()
         quantise_x(1)
         quantise_x(2)
         matmuls(0, LSD)
@@ -527,16 +527,16 @@ def tile_chainlveg_pa_kernel(
         m1m_turn()
         regroup_scalar(W2)
         load_sigmoid_table()
-        evict(0, LSD, "v", 0)
         regroup_vector(M0)
+        evict(0, LSD, "v", 0)
         evict(0, LSD, "v", 1)
         evict(0, LSD, "v", 2)
         regroup_vector(M1)
         quantise_w(W0)
-        quantise_w(W1)
-        matmuls(1, LSD)
         quantise_w(M0)
         clip_v(0)
+        quantise_w(W1)
+        matmuls(1, LSD)
         quantise_w(M1)
         diff_v(0)
         sigmoid(0, -2.0)

@@ -34,7 +34,8 @@ def tile_chainlveg_pa_kernel(
     with ExitStack() as ctx:
         const = ctx.enter_context(tc.tile_pool(name="const", bufs=1))
         work = ctx.enter_context(tc.tile_pool(name="work", bufs=2))
-        psum = ctx.enter_context(tc.psum_pool(name="psum", bufs=8))
+        psum = ctx.enter_context(tc.psum_pool(name="psum", bufs=7))
+        psum_keep = ctx.enter_context(tc.psum_pool(name="psum_keep", bufs=1))
         ctx.enter_context(tc.manual_schedule())
 
         x_rows = x.rearrange("b p d -> (b p) d").rearrange("(t q) d -> q t d", q=P)
@@ -67,6 +68,7 @@ def tile_chainlveg_pa_kernel(
         m1m_cols = const.tile([P, MT * P], F32, name="m1m_cols")
         twocol = const.tile([P, 1], F32, name="twocol")
         ie1e = const.tile([P, MT, 64], F32, name="ie1e")
+        ie1_keep = psum_keep.tile([P, MT, 64], F32, name="ie1_keep")
         vsum = const.tile([P, MT * 16], F32, name="vsum")
         t0 = const.tile([P, MT * 16], F32, name="t0")
         xg = const.tile([P, MT, K], BF16, name="xg", align_bytes=64)
@@ -126,12 +128,20 @@ def tile_chainlveg_pa_kernel(
                 )
             nc.scalar.copy(out=m1m_cols[:], in_=tp[:])
 
+        def table_ie1e():
+            nc.vector.tensor_copy(out=as_jtg(ie1e), in_=spread_t(ie1s[:]))
+
+        def keep_ie1e():
+            nc.tensor.matmul(
+                out=ie1_keep[:].rearrange("p m c -> p (m c)"), lhsT=ident[:],
+                rhs=ie1e[:].rearrange("p m c -> p (m c)"), start=True, stop=True,
+            )
+
         def tables_rest():
             sv_pairs = sv_flat.rearrange("p (a g) -> p a g", g=2)
             nc.vector.tensor_tensor(
                 out=vsum[:], in0=sv_pairs[:, :, 0], in1=sv_pairs[:, :, 1], op=ALU.add
             )
-            nc.vector.tensor_copy(out=as_jtg(ie1e), in_=spread_t(ie1s[:]))
             nc.vector.scalar_tensor_tensor(
                 out=t0[:],
                 in0=sw[:].rearrange("p m c -> p (m c)"),
@@ -396,14 +406,23 @@ def tile_chainlveg_pa_kernel(
                 )
                 nc.sync.dma_start(out=mu_rows[:, mt, cols(h, NH)], in_=t[("a", h)][:, mt, :])
 
+        def mean_out_pool(h, mt):
+            if mt == 0:
+                new("mu", h)
+            nc.gpsimd.tensor_tensor(
+                out=by_i1(t[("mu", h)], mt), in0=one_i(m1e, mt, 64), in1=by_i1(t[("a", h)], mt),
+                op=ALU.subtract,
+            )
+            nc.sync.dma_start(out=mu_rows[:, mt, cols(h, NH)], in_=t[("mu", h)][:, mt, :])
+
         def prod_q2(h, mt=None):
             if mt is None:
                 nc.vector.tensor_tensor(
-                    out=by_i(t[("q", h)]), in0=by_i(t[("q", h)]), in1=all_i(ie1e, 64), op=ALU.mult
+                    out=by_i(t[("q", h)]), in0=by_i(t[("q", h)]), in1=all_i(ie1_keep, 64), op=ALU.mult
                 )
             else:
                 nc.vector.tensor_tensor(
-                    out=by_i1(t[("q", h)], mt), in0=by_i1(t[("q", h)], mt), in1=one_i(ie1e, mt, 64),
+                    out=by_i1(t[("q", h)], mt), in0=by_i1(t[("q", h)], mt), in1=one_i(ie1_keep, mt, 64),
                     op=ALU.mult,
                 )
 
@@ -511,12 +530,15 @@ def tile_chainlveg_pa_kernel(
         x_turn(0)
         table_m1m()
         table_m1m_rows()
+        table_m1e()
+        table_ie1e()
         regroup_both(V1)
         x_turn(1)
         quantise_x(0)
         x_turn(2)
         quantise_w(V0)
         bias_turn()
+        keep_ie1e()
         quantise_w(V1)
         spread_bias()
         quantise_x(1)
@@ -552,7 +574,6 @@ def tile_chainlveg_pa_kernel(
         quantise_w(W3)
         diff_v(1)
         sigmoid(1, -2.0)
-        table_m1e()
         tables_rest()
         table_neghalf()
         table_te_rows()
@@ -561,10 +582,11 @@ def tile_chainlveg_pa_kernel(
         mean_clipped(1)
         log_rho(1, 1.0)
         prod_a(0)
+        for mt in range(MT):
+            mean_out_pool(0, mt)
         prod_q1(0)
         for nt in range(4):
             mean_turn(1, nt)
-        mean_out(0)
         prod_q2(0)
         var_out(0)
         pair_sum_open(0)
@@ -572,6 +594,8 @@ def tile_chainlveg_pa_kernel(
         for mt in range(MT):
             pair_sum_close(0, mt)
         prod_a(1)
+        for mt in range(MT):
+            mean_out_pool(1, mt)
         prod_q1(1)
         for mt in range(MT):
             scale_out_scalar(0, mt)
@@ -582,7 +606,6 @@ def tile_chainlveg_pa_kernel(
             sum_z(1, mt)
             pair_sum_close(1, mt)
         for mt in range(MT):
-            mean_out(1, mt)
             var_out(1, mt)
         for mt in range(MT):
             scale_out_scalar(1, mt)

@@ -58,6 +58,7 @@ def tile_chainlveg_pa_kernel(
         onecol = const.tile([P, 1], F32, name="onecol")
         dummy = const.tile([P, 1], F32, name="dummy")
         neghalf = const.tile([P, P], F32, name="neghalf")
+        poshalf = const.tile([P, P], F32, name="poshalf")
         te_rows = const.tile([P, MT, P], F32, name="te_rows")
         te_cols = const.tile([P, MT, P], F32, name="te_cols")
         ie1s = const.tile([P, MT * 32], F32, name="ie1s")
@@ -156,10 +157,9 @@ def tile_chainlveg_pa_kernel(
                 out=te_rows[:, :, 0:32].rearrange("p m (j t) -> p m j t", t=2),
                 in_=t0[:].rearrange("p (m j) -> p m j", m=MT).unsqueeze(3).to_broadcast([P, MT, 16, 2]),
             )
-
-        def table_neghalf():
-            nc.vector.tensor_scalar(
-                out=neghalf[:], in0=ident[:], scalar1=-0.5, scalar2=None, op0=ALU.mult
+            nc.vector.tensor_copy(
+                out=te_rows[:, :, 32:P].rearrange("p m (r c) -> p m r c", r=3),
+                in_=te_rows[:, :, 0:32].unsqueeze(2).to_broadcast([P, MT, 3, 32]),
             )
 
         def te_turn():
@@ -463,11 +463,20 @@ def tile_chainlveg_pa_kernel(
         def pair_sum_open(h):
             for mt in range(MT):
                 zps[(h, mt)] = psum.tile([P, NH // 2], F32, name="zp_%d_%d" % (h, mt), tag="bank")
+                for b in range(2):
+                    nc.tensor.matmul(
+                        out=zps[(h, mt)][:, b * P : (b + 1) * P], lhsT=te_cols[:, mt, :], rhs=ident[:],
+                        is_transpose=True, start=(b == 0), stop=False,
+                    )
+
+        def plane(a, mt, g):
+            return a[:, mt, :].rearrange("p (c g) -> p g c", g=2)[:, g, :]
+
+        def pair_sum_terms(h, mt, kind, last):
+            for g in range(2):
                 nc.tensor.matmul(
-                    out=zps[(h, mt)][:].rearrange("p (i c) -> p i c", i=NI),
-                    lhsT=te_cols[:, mt, :],
-                    rhs=ident[:, 0:32].unsqueeze(1).to_broadcast([P, NI, 32]),
-                    start=True, stop=False,
+                    out=zps[(h, mt)][:], lhsT=(neghalf if kind == "q" else poshalf)[:],
+                    rhs=plane(t[(kind, h)], mt, g), start=False, stop=(last and g == 1),
                 )
 
         def pair_sum_close(h, mt):
@@ -522,7 +531,10 @@ def tile_chainlveg_pa_kernel(
         make_identity(nc, ident[:])
         nc.gpsimd.memset(onecol[:], 1.0)
         nc.gpsimd.memset(twocol[:], 2.0)
-        nc.gpsimd.memset(te_rows[:], 0.0)
+        for sign, half_ident in ((-0.5, neghalf), (0.5, poshalf)):
+            nc.gpsimd.tensor_scalar(
+                out=half_ident[:], in0=ident[:], scalar1=sign, scalar2=0.0, op0=ALU.mult, op1=ALU.add
+            )
         nc.scalar.activation(out=ie1s[:], in_=sv_flat, func=ACT.Exp, scale=-2.0)
 
         table_v1()
@@ -563,23 +575,31 @@ def tile_chainlveg_pa_kernel(
         diff_v(0)
         sigmoid(0, -2.0)
         mean_clipped(0)
-        regroup_vector(W3)
         evict(1, LSD, "v", 0)
         evict(1, LSD, "v", 1)
         evict(1, LSD, "v", 2)
-        for nt in range(4):
-            mean_turn(0, nt)
+        regroup_vector(W3)
         quantise_w(W2)
-        clip_v(1)
+        mean_turn(0, 0)
+        mean_turn(0, 1)
         quantise_w(W3)
+        mean_products(1, 0)
+        mean_products(1, 1)
+        mean_turn(0, 2)
+        mean_turn(0, 3)
+        clip_v(1)
+        mean_upper(1, 0)
+        mean_products(1, 2)
+        mean_upper(1, 1)
+        mean_products(1, 3)
+        mean_upper(1, 2)
+        mean_upper(1, 3)
+        tables_rest()
         diff_v(1)
         sigmoid(1, -2.0)
-        tables_rest()
-        table_neghalf()
         table_te_rows()
-        log_rho(0, 1.0)
         te_turn()
-        mean_clipped(1)
+        log_rho(0, 1.0)
         log_rho(1, 1.0)
         prod_a(0)
         for mt in range(MT):
@@ -587,25 +607,23 @@ def tile_chainlveg_pa_kernel(
         prod_q1(0)
         for nt in range(4):
             mean_turn(1, nt)
-        prod_q2(0)
-        var_out(0)
         pair_sum_open(0)
-        sum_z(0)
         for mt in range(MT):
-            pair_sum_close(0, mt)
+            prod_q2(0, mt)
+            pair_sum_terms(0, mt, "q", False)
         prod_a(1)
         for mt in range(MT):
             mean_out_pool(1, mt)
         prod_q1(1)
-        for mt in range(MT):
-            scale_out_scalar(0, mt)
         pair_sum_open(1)
         for mt in range(MT):
             prod_q2(1, mt)
         for mt in range(MT):
+            pair_sum_terms(0, mt, "lr", True)
+        for mt in range(MT):
             sum_z(1, mt)
             pair_sum_close(1, mt)
-        for mt in range(MT):
-            var_out(1, mt)
-        for mt in range(MT):
-            scale_out_scalar(1, mt)
+        for h in range(H):
+            for mt in range(MT):
+                var_out(h, mt)
+                scale_out_scalar(h, mt)

@@ -138,11 +138,13 @@ def tile_chainlveg_pa_kernel(
                 rhs=ie1e[:].rearrange("p m c -> p (m c)"), start=True, stop=True,
             )
 
-        def tables_rest():
+        def table_vsum():
             sv_pairs = sv_flat.rearrange("p (a g) -> p a g", g=2)
             nc.vector.tensor_tensor(
                 out=vsum[:], in0=sv_pairs[:, :, 0], in1=sv_pairs[:, :, 1], op=ALU.add
             )
+
+        def table_t0():
             nc.vector.scalar_tensor_tensor(
                 out=t0[:],
                 in0=sw[:].rearrange("p m c -> p (m c)"),
@@ -152,11 +154,13 @@ def tile_chainlveg_pa_kernel(
                 op1=ALU.subtract,
             )
 
-        def table_te_rows():
+        def table_te_first():
             nc.vector.tensor_copy(
                 out=te_rows[:, :, 0:32].rearrange("p m (j t) -> p m j t", t=2),
                 in_=t0[:].rearrange("p (m j) -> p m j", m=MT).unsqueeze(3).to_broadcast([P, MT, 16, 2]),
             )
+
+        def table_te_rest():
             nc.vector.tensor_copy(
                 out=te_rows[:, :, 32:P].rearrange("p m (r c) -> p m r c", r=3),
                 in_=te_rows[:, :, 0:32].unsqueeze(2).to_broadcast([P, MT, 3, 32]),
@@ -225,7 +229,10 @@ def tile_chainlveg_pa_kernel(
             nc.tensor.transpose(out=btp[:], in_=btile[:], identity=identb[:])
             nc.vector.tensor_copy(out=bcols[:], in_=btp[:, 0:16])
             nc.vector.tensor_scalar(
-                out=bm1[:], in0=btp[:, 0:8], scalar1=1.0, scalar2=None, op0=ALU.add
+                out=bm1[:, 0:4], in0=btp[:, 0:4], scalar1=1.0, scalar2=None, op0=ALU.add
+            )
+            nc.vector.tensor_scalar(
+                out=bm1[:, 4:8], in0=btp[:, 4:8], scalar1=-1.0, scalar2=1.0, op0=ALU.mult, op1=ALU.add
             )
 
         def spread_bias():
@@ -276,7 +283,13 @@ def tile_chainlveg_pa_kernel(
                     )
             nc.scalar.activation(
                 out=t[("m", h)][:, nt, :], in_=at[:], func=ACT.Relu,
-                bias=bm1[:, h * 4 + nt : h * 4 + nt + 1], scale=1.0,
+                bias=bm1[:, h * 4 + nt : h * 4 + nt + 1], scale=(1.0, -1.0)[h],
+            )
+
+        def mean_upper_pool(h, nt):
+            nc.gpsimd.tensor_scalar(
+                out=t[("m", h)][:, nt, :], in0=t[("m", h)][:, nt, :], scalar1=2.0, scalar2=0.0,
+                op0=ALU.min, op1=ALU.add,
             )
 
         def mean_upper(h, nt):
@@ -541,17 +554,21 @@ def tile_chainlveg_pa_kernel(
         regroup_both(V0)
         x_turn(0)
         table_m1m()
-        table_m1m_rows()
         table_m1e()
         table_ie1e()
+        table_vsum()
+        table_m1m_rows()
         regroup_both(V1)
         x_turn(1)
         quantise_x(0)
+        table_t0()
         x_turn(2)
         quantise_w(V0)
+        table_te_first()
         bias_turn()
         keep_ie1e()
         quantise_w(V1)
+        table_te_rest()
         spread_bias()
         quantise_x(1)
         quantise_x(2)
@@ -559,6 +576,7 @@ def tile_chainlveg_pa_kernel(
         regroup_scalar(W0)
         regroup_scalar(W1)
         m1m_turn()
+        te_turn()
         regroup_scalar(W2)
         load_sigmoid_table()
         regroup_vector(M0)
@@ -572,9 +590,9 @@ def tile_chainlveg_pa_kernel(
         quantise_w(W1)
         matmuls(1, LSD)
         quantise_w(M1)
+        mean_clipped(0)
         diff_v(0)
         sigmoid(0, -2.0)
-        mean_clipped(0)
         evict(1, LSD, "v", 0)
         evict(1, LSD, "v", 1)
         evict(1, LSD, "v", 2)
@@ -588,17 +606,14 @@ def tile_chainlveg_pa_kernel(
         mean_turn(0, 2)
         mean_turn(0, 3)
         clip_v(1)
-        mean_upper(1, 0)
+        mean_upper_pool(1, 0)
         mean_products(1, 2)
-        mean_upper(1, 1)
+        mean_upper_pool(1, 1)
         mean_products(1, 3)
-        mean_upper(1, 2)
-        mean_upper(1, 3)
-        tables_rest()
+        mean_upper_pool(1, 2)
+        mean_upper_pool(1, 3)
         diff_v(1)
         sigmoid(1, -2.0)
-        table_te_rows()
-        te_turn()
         log_rho(0, 1.0)
         log_rho(1, 1.0)
         prod_a(0)

@@ -82,9 +82,26 @@ def tile_chainlveg_pa_kernel(
         pieces = [(h, w, c) for h in range(H) for w in (LSD, MEAN) for c in range(KP)]
         raw = {}
         grouped = {}
+        chain_of = {(1, LSD, 1): "chain_a", (1, MEAN, 1): "chain_b"}
         for key in pieces:
-            raw[key] = const.tile([P, 4, NH], BF16, name="raw_%d_%d_%d" % key)
-            grouped[key] = const.tile([P, NH, 4], BF16, name="grp_%d_%d_%d" % key, align_bytes=64)
+            if key == (0, MEAN, 0):
+                raw[key] = const.tile([P, 4, NH], BF16, name="raw_%d_%d_%d" % key, tag="chain_a", align_bytes=64)
+            else:
+                raw[key] = const.tile([P, 4, NH], BF16, name="raw_%d_%d_%d" % key)
+            if key == (0, MEAN, 1):
+                grouped[key] = const.tile([P, NH, 4], BF16, name="grp_%d_%d_%d" % key, tag="chain_b", align_bytes=64)
+            elif key not in chain_of:
+                grouped[key] = const.tile([P, NH, 4], BF16, name="grp_%d_%d_%d" % key, align_bytes=64)
+
+        def regroup_pool(key, c1):
+            grouped[key] = const.tile(
+                [P, NH, 4], BF16, name="grp_%d_%d_%d" % key, tag=chain_of[key], align_bytes=64
+            )
+            nc.gpsimd.tensor_scalar(
+                out=grouped[key][:, 0:c1, :].rearrange("p (c i) t -> p c t i", i=4),
+                in0=raw[key][:, :, 0:c1].rearrange("p t (c i) -> p c t i", i=4),
+                scalar1=1.0, scalar2=0.0, op0=ALU.mult, op1=ALU.add,
+            )
 
         def load_x(mt):
             nc.sync.dma_start(out=x_sb[:, mt, :], in_=x_rows[:, mt, :])
@@ -229,10 +246,7 @@ def tile_chainlveg_pa_kernel(
             nc.tensor.transpose(out=btp[:], in_=btile[:], identity=identb[:])
             nc.vector.tensor_copy(out=bcols[:], in_=btp[:, 0:16])
             nc.vector.tensor_scalar(
-                out=bm1[:, 0:4], in0=btp[:, 0:4], scalar1=1.0, scalar2=None, op0=ALU.add
-            )
-            nc.vector.tensor_scalar(
-                out=bm1[:, 4:8], in0=btp[:, 4:8], scalar1=-1.0, scalar2=1.0, op0=ALU.mult, op1=ALU.add
+                out=bm1[:], in0=btp[:, 0:8], scalar1=1.0, scalar2=None, op0=ALU.add
             )
 
         def spread_bias():
@@ -283,13 +297,7 @@ def tile_chainlveg_pa_kernel(
                     )
             nc.scalar.activation(
                 out=t[("m", h)][:, nt, :], in_=at[:], func=ACT.Relu,
-                bias=bm1[:, h * 4 + nt : h * 4 + nt + 1], scale=(1.0, -1.0)[h],
-            )
-
-        def mean_upper_pool(h, nt):
-            nc.gpsimd.tensor_scalar(
-                out=t[("m", h)][:, nt, :], in0=t[("m", h)][:, nt, :], scalar1=2.0, scalar2=0.0,
-                op0=ALU.min, op1=ALU.add,
+                bias=bm1[:, h * 4 + nt : h * 4 + nt + 1], scale=1.0,
             )
 
         def mean_upper(h, nt):
@@ -574,12 +582,13 @@ def tile_chainlveg_pa_kernel(
         quantise_x(2)
         matmuls(0, LSD)
         regroup_scalar(W0)
-        regroup_scalar(W1)
+        regroup_vector(M0)
+        regroup_pool(W1, NH // 2)
+        regroup_scalar(W1, 1)
         m1m_turn()
         te_turn()
         regroup_scalar(W2)
         load_sigmoid_table()
-        regroup_vector(M0)
         evict(0, LSD, "v", 0)
         evict(0, LSD, "v", 1)
         evict(0, LSD, "v", 2)
@@ -590,13 +599,14 @@ def tile_chainlveg_pa_kernel(
         quantise_w(W1)
         matmuls(1, LSD)
         quantise_w(M1)
+        regroup_pool(W3, NH // 2)
         mean_clipped(0)
-        diff_v(0)
-        sigmoid(0, -2.0)
         evict(1, LSD, "v", 0)
         evict(1, LSD, "v", 1)
         evict(1, LSD, "v", 2)
-        regroup_vector(W3)
+        diff_v(0)
+        sigmoid(0, -2.0)
+        regroup(nc.vector.tensor_copy, W3, NH // 2, NH)
         quantise_w(W2)
         mean_turn(0, 0)
         mean_turn(0, 1)
@@ -606,12 +616,12 @@ def tile_chainlveg_pa_kernel(
         mean_turn(0, 2)
         mean_turn(0, 3)
         clip_v(1)
-        mean_upper_pool(1, 0)
+        mean_upper(1, 0)
         mean_products(1, 2)
-        mean_upper_pool(1, 1)
+        mean_upper(1, 1)
         mean_products(1, 3)
-        mean_upper_pool(1, 2)
-        mean_upper_pool(1, 3)
+        mean_upper(1, 2)
+        mean_upper(1, 3)
         diff_v(1)
         sigmoid(1, -2.0)
         log_rho(0, 1.0)

@@ -73,8 +73,8 @@ def tile_chainlveg_pa_kernel(
         vsum = const.tile([P, MT * 16], F32, name="vsum")
         t0 = const.tile([P, MT * 16], F32, name="t0")
         xg = const.tile([P, MT, K], BF16, name="xg", align_bytes=64)
-        xq = const.tile([P, KP, MT * P], U32, name="xq", align_bytes=64)
-        xs = const.tile([P, KP, MT * P], U8, name="xs", align_bytes=64)
+        xq = const.tile([P, KP, NH], U32, name="xq", align_bytes=64)
+        xs = const.tile([P, KP, NH], U8, name="xs", align_bytes=64)
         bm1 = const.tile([P, 8], F32, name="bm1")
         wq = const.tile([P, 8, NH], U32, name="wq", align_bytes=64)
         ws = const.tile([P, 8, NH], U8, name="ws", align_bytes=64)
@@ -282,21 +282,20 @@ def tile_chainlveg_pa_kernel(
         def mean_products(h, nt):
             if nt == 0:
                 t[("m", h)] = work.tile([P, 4, MT * P], F32, name="m_%d" % h, tag="m")
-            at = psum.tile([P, MT * P], F32, name="at_%d_%d" % (h, nt), tag="bank")
-            for r0, r1 in ((0, 2 * P), (2 * P, 3 * P)):
-                for c in range(KP):
-                    i = pieces.index((h, MEAN, c))
-                    nc.tensor.matmul_mx(
-                        out=at[:, r0:r1],
-                        lhsT=wq[:, i, nt * P : (nt + 1) * P].bitcast(FP8X4),
-                        lhsT_scale=ws[:, i, nt * P : (nt + 1) * P],
-                        rhs=xq[:, c, r0:r1].bitcast(FP8X4),
-                        rhs_scale=xs[:, c, r0:r1],
-                        start=(c == 0),
-                        stop=(c == KP - 1),
-                    )
+            at = psum.tile([P, NH], F32, name="at_%d_%d" % (h, nt), tag="bank")
+            for c in range(KP):
+                i = pieces.index((h, MEAN, c))
+                nc.tensor.matmul_mx(
+                    out=at[:],
+                    lhsT=wq[:, i, nt * P : (nt + 1) * P].bitcast(FP8X4),
+                    lhsT_scale=ws[:, i, nt * P : (nt + 1) * P],
+                    rhs=xq[:, c, :].bitcast(FP8X4),
+                    rhs_scale=xs[:, c, :],
+                    start=(c == 0),
+                    stop=(c == KP - 1),
+                )
             nc.scalar.activation(
-                out=t[("m", h)][:, nt, :], in_=at[:], func=ACT.Relu,
+                out=t[("m", h)][:, nt, :], in_=at[:, 0 : MT * P], func=ACT.Relu,
                 bias=bm1[:, h * 4 + nt : h * 4 + nt + 1], scale=1.0,
             )
 
@@ -558,6 +557,8 @@ def tile_chainlveg_pa_kernel(
             )
         nc.scalar.activation(out=ie1s[:], in_=sv_flat, func=ACT.Exp, scale=-2.0)
 
+        nc.vector.memset(xq[:, :, MT * P : NH].bitcast(I32), 0)
+        nc.vector.memset(xs[:, :, MT * P : NH].bitcast(I32), 0)
         table_v1()
         regroup_both(V0)
         x_turn(0)

@@ -435,6 +435,12 @@ def tile_chainlveg_pa_kernel(
             )
             nc.sync.dma_start(out=mu_rows[:, mt, cols(h, NH)], in_=t[("mu", h)][:, mt, :])
 
+        def prod_q2_pool(h, mt):
+            nc.gpsimd.tensor_tensor(
+                out=by_i1(t[("q", h)], mt), in0=by_i1(t[("q", h)], mt), in1=one_i(ie1e, mt, 64),
+                op=ALU.mult,
+            )
+
         def prod_q2(h, mt=None):
             if mt is None:
                 nc.vector.tensor_tensor(
@@ -634,9 +640,11 @@ def tile_chainlveg_pa_kernel(
         for nt in range(4):
             mean_turn(1, nt)
         pair_sum_open(0)
-        for mt in range(MT):
+        prod_q2_pool(0, 2)
+        for mt in range(MT - 1):
             prod_q2(0, mt)
             pair_sum_terms(0, mt, "q", False)
+        pair_sum_terms(0, 2, "q", False)
         prod_a(1)
         for mt in range(MT):
             mean_out_pool(1, mt)

@@ -82,15 +82,13 @@ def tile_chainlveg_pa_kernel(
         pieces = [(h, w, c) for h in range(H) for w in (LSD, MEAN) for c in range(KP)]
         raw = {}
         grouped = {}
-        chain_of = {(1, LSD, 1): "chain_a", (1, MEAN, 1): "chain_b"}
+        chain_of = {(0, MEAN, 1): "chain_a", (1, MEAN, 1): "chain_a"}
         for key in pieces:
             if key == (0, MEAN, 0):
                 raw[key] = const.tile([P, 4, NH], BF16, name="raw_%d_%d_%d" % key, tag="chain_a", align_bytes=64)
             else:
                 raw[key] = const.tile([P, 4, NH], BF16, name="raw_%d_%d_%d" % key)
-            if key == (0, MEAN, 1):
-                grouped[key] = const.tile([P, NH, 4], BF16, name="grp_%d_%d_%d" % key, tag="chain_b", align_bytes=64)
-            elif key not in chain_of:
+            if key not in chain_of:
                 grouped[key] = const.tile([P, NH, 4], BF16, name="grp_%d_%d_%d" % key, align_bytes=64)
 
         def regroup_pool(key, c1):
@@ -551,7 +549,7 @@ def tile_chainlveg_pa_kernel(
         load_w(V1)
         load_x(1)
         load_x(2)
-        for key in (W0, M0, W1, M1, W2, W3):
+        for key in (W0, M0, M1, W1, W2, W3):
             load_w(key)
         make_identity(nc, identb[:])
         make_identity(nc, ident[:])
@@ -590,8 +588,8 @@ def tile_chainlveg_pa_kernel(
         matmuls(0, LSD)
         regroup_scalar(W0)
         regroup_vector(M0)
-        regroup_pool(W1, NH // 2)
-        regroup_scalar(W1, 1)
+        regroup_pool(M1, NH // 2)
+        regroup_scalar(W1)
         m1m_turn()
         te_turn()
         regroup_scalar(W2)
@@ -599,7 +597,7 @@ def tile_chainlveg_pa_kernel(
         evict(0, LSD, "v", 0)
         evict(0, LSD, "v", 1)
         evict(0, LSD, "v", 2)
-        regroup_vector(M1)
+        regroup(nc.vector.tensor_copy, M1, NH // 2, NH)
         quantise_w(W0)
         quantise_w(M0)
         clip_v(0)

@@ -61,7 +61,9 @@ def tile_chainlveg_pa_kernel(
         poshalf = const.tile([P, P], F32, name="poshalf")
         te_rows = const.tile([P, MT, P], F32, name="te_rows")
         te_cols = const.tile([P, MT, P], F32, name="te_cols")
-        ie1s = const.tile([P, MT * 32], F32, name="ie1s")
+        sig_neg = const.tile([P, MT * 32], F32, name="sig_neg")
+        sig_pos = const.tile([P, MT * 32], F32, name="sig_pos")
+        inv_pos = const.tile([P, MT * 32], F32, name="inv_pos")
         v1e = const.tile([P, MT, 64], F32, name="v1e")
         m1e = const.tile([P, MT, 64], F32, name="m1e")
         m1m = const.tile([P, MT, 64], F32, name="m1m")
@@ -144,8 +146,13 @@ def tile_chainlveg_pa_kernel(
                 )
             nc.scalar.copy(out=m1m_cols[:], in_=tp[:])
 
+        def table_inv_pos():
+            nc.vector.reciprocal(out=inv_pos[:], in_=sig_pos[:])
+
         def table_ie1e():
-            nc.vector.tensor_copy(out=as_jtg(ie1e), in_=spread_t(ie1s[:]))
+            nc.vector.tensor_tensor(
+                out=as_jtg(ie1e), in0=spread_t(sig_neg[:]), in1=spread_t(inv_pos[:]), op=ALU.mult
+            )
 
         def keep_ie1e():
             nc.tensor.matmul(
@@ -538,12 +545,14 @@ def tile_chainlveg_pa_kernel(
 
         V0, V1, M0, M1 = (0, LSD, 0), (0, LSD, 1), (0, MEAN, 0), (0, MEAN, 1)
         W0, W1, W2, W3 = (1, LSD, 0), (1, LSD, 1), (1, MEAN, 0), (1, MEAN, 1)
+        nc.gpsimd.memset(onecol[:], 1.0)
         nc.scalar.dma_start(out=sv[:], in_=sv_rows)
         nc.scalar.dma_start(out=sm[:], in_=sm_rows)
         nc.scalar.dma_start(out=sw[:], in_=sw_rows)
         nc.gpsimd.memset(btile[:], 0.0)
         nc.scalar.dma_start(out=btile[0:8, :], in_=tcm_b.rearrange("(r c) -> r c", c=P))
         nc.scalar.dma_start(out=btile[8:16, :], in_=tcv_b.rearrange("(r c) -> r c", c=P))
+        load_sigmoid_table()
         load_w(V0)
         load_x(0)
         load_w(V1)
@@ -553,17 +562,18 @@ def tile_chainlveg_pa_kernel(
             load_w(key)
         make_identity(nc, identb[:])
         make_identity(nc, ident[:])
-        nc.gpsimd.memset(onecol[:], 1.0)
         nc.gpsimd.memset(twocol[:], 2.0)
         for sign, half_ident in ((-0.5, neghalf), (0.5, poshalf)):
             nc.gpsimd.tensor_scalar(
                 out=half_ident[:], in0=ident[:], scalar1=sign, scalar2=0.0, op0=ALU.mult, op1=ALU.add
             )
-        nc.scalar.activation(out=ie1s[:], in_=sv_flat, func=ACT.Exp, scale=-2.0)
+        nc.scalar.activation(out=sig_pos[:], in_=sv_flat, func=ACT.Sigmoid, scale=2.0)
+        nc.scalar.activation(out=sig_neg[:], in_=sv_flat, func=ACT.Sigmoid, scale=-2.0)
 
         nc.vector.memset(xq[:, :, MT * P : NH].bitcast(I32), 0)
         nc.vector.memset(xs[:, :, MT * P : NH].bitcast(I32), 0)
         table_v1()
+        table_inv_pos()
         regroup_both(V0)
         x_turn(0)
         table_m1m()
@@ -593,7 +603,6 @@ def tile_chainlveg_pa_kernel(
         m1m_turn()
         te_turn()
         regroup_scalar(W2)
-        load_sigmoid_table()
         evict(0, LSD, "v", 0)
         evict(0, LSD, "v", 1)
         evict(0, LSD, "v", 2)

@@ -93,6 +93,8 @@ def tile_chainlveg_pa_kernel(
             if key not in chain_of:
                 grouped[key] = const.tile([P, NH, 4], BF16, name="grp_%d_%d_%d" % key, align_bytes=64)
 
+        upper_half = const.tile([P, NH // 2, 4], BF16, name="upper_half", align_bytes=64)
+
         def regroup_pool(key, c1):
             grouped[key] = const.tile(
                 [P, NH, 4], BF16, name="grp_%d_%d_%d" % key, tag=chain_of[key], align_bytes=64
@@ -245,6 +247,21 @@ def tile_chainlveg_pa_kernel(
                 scales=ws[:, i, :],
                 in_=grouped[key][:].rearrange("p w j -> p (w j)"),
             )
+
+        def regroup_upper_scalar(key):
+            nc.scalar.copy(
+                out=upper_half[:].rearrange("p (c i) t -> p c t i", i=4),
+                in_=raw[key][:, :, NH // 2 : NH].rearrange("p t (c i) -> p c t i", i=4),
+            )
+
+        def quantise_w_halves(key):
+            i = pieces.index(key)
+            for lo, src in ((0, grouped[key][:, 0 : NH // 2, :]), (NH // 2, upper_half[:])):
+                nc.vector.quantize_mx(
+                    out=wq[:, i, lo : lo + NH // 2].bitcast(FP8X4),
+                    scales=ws[:, i, lo : lo + NH // 2],
+                    in_=src.rearrange("p w j -> p (w j)"),
+                )
 
         def bias_turn():
             btp = psum.tile([P, P], BF16, name="btp", tag="bank")
@@ -603,6 +620,7 @@ def tile_chainlveg_pa_kernel(
         m1m_turn()
         te_turn()
         regroup_scalar(W2)
+        regroup_upper_scalar(W3)
         evict(0, LSD, "v", 0)
         evict(0, LSD, "v", 1)
         evict(0, LSD, "v", 2)
@@ -620,11 +638,10 @@ def tile_chainlveg_pa_kernel(
         evict(1, LSD, "v", 2)
         diff_v(0)
         sigmoid(0, -2.0)
-        regroup(nc.vector.tensor_copy, W3, NH // 2, NH)
         quantise_w(W2)
         mean_turn(0, 0)
         mean_turn(0, 1)
-        quantise_w(W3)
+        quantise_w_halves(W3)
         mean_products(1, 0)
         mean_products(1, 1)
         mean_turn(0, 2)

@@ -100,8 +100,8 @@ def tile_chainlveg_pa_kernel(
                 [P, NH, 4], BF16, name="grp_%d_%d_%d" % key, tag=chain_of[key], align_bytes=64
             )
             nc.gpsimd.tensor_scalar(
-                out=grouped[key][:, 0:c1, :].rearrange("p (c i) t -> p c t i", i=4),
-                in0=raw[key][:, :, 0:c1].rearrange("p t (c i) -> p c t i", i=4),
+                out=grouped[key][:, 0:c1, :],
+                in0=raw[key][:, :, 0:c1].rearrange("p t c -> p c t"),
                 scalar1=1.0, scalar2=0.0, op0=ALU.mult, op1=ALU.add,
             )
 

@@ -380,6 +380,20 @@ def tile_chainlveg_pa_kernel(
         def by_i1(a, mt):
             return a[:, mt, :].rearrange("p (i c) -> p i c", i=NI)
 
+        def pairs(ap):
+            return ap.rearrange("p (c g) -> p c g", g=2)
+
+        def planes(ap):
+            return ap.rearrange("p (g c) -> p c g", g=2)
+
+        def by_gi(a, mt):
+            return a[:, mt, :].rearrange("p (g i c) -> p g i c", g=2, i=NI)
+
+        def table_gi(tab, mt):
+            return (
+                tab[:, mt, :].rearrange("p (c g) -> p g c", g=2).unsqueeze(2).to_broadcast([P, 2, NI, 32])
+            )
+
         def flat(a):
             return a[:].rearrange("p m c -> p (m c)")
 
@@ -413,7 +427,8 @@ def tile_chainlveg_pa_kernel(
 
         def log_rho(h, scale):
             nc.scalar.activation(
-                out=flat(new("lr", h)), in_=flat(t[("rho", h)]), func=ACT.Ln, scale=scale
+                out=new("lr", h)[:].rearrange("p m (g c) -> p m c g", g=2),
+                in_=t[("rho", h)][:].rearrange("p m (c g) -> p m c g", g=2), func=ACT.Ln, scale=scale,
             )
 
         def cols(h, width):
@@ -431,8 +446,8 @@ def tile_chainlveg_pa_kernel(
             new("q", h)
             for mt in range(MT):
                 nc.vector.tensor_tensor(
-                    out=t[("q", h)][:, mt, :], in0=arow[(h, mt)][:], in1=t[("a", h)][:, mt, :],
-                    op=ALU.mult,
+                    out=planes(t[("q", h)][:, mt, :]), in0=pairs(arow[(h, mt)][:]),
+                    in1=pairs(t[("a", h)][:, mt, :]), op=ALU.mult,
                 )
 
         def mean_out(h, mt=None):
@@ -459,7 +474,7 @@ def tile_chainlveg_pa_kernel(
 
         def prod_q2_pool(h, mt):
             nc.gpsimd.tensor_tensor(
-                out=by_i1(t[("q", h)], mt), in0=by_i1(t[("q", h)], mt), in1=one_i(ie1e, mt, 64),
+                out=by_gi(t[("q", h)], mt), in0=by_gi(t[("q", h)], mt), in1=table_gi(ie1e, mt),
                 op=ALU.mult,
             )
 
@@ -470,7 +485,7 @@ def tile_chainlveg_pa_kernel(
                 )
             else:
                 nc.vector.tensor_tensor(
-                    out=by_i1(t[("q", h)], mt), in0=by_i1(t[("q", h)], mt), in1=one_i(ie1_keep, mt, 64),
+                    out=by_gi(t[("q", h)], mt), in0=by_gi(t[("q", h)], mt), in1=table_gi(ie1_keep, mt),
                     op=ALU.mult,
                 )
 
@@ -486,10 +501,8 @@ def tile_chainlveg_pa_kernel(
                 )
             else:
                 nc.vector.tensor_tensor(
-                    out=t[("z", h)][:, mt, :, :].rearrange("p g c -> p c g"),
-                    in0=t[("q", h)][:, mt, :].rearrange("p (c g) -> p c g", g=2),
-                    in1=t[("lr", h)][:, mt, :].rearrange("p (c g) -> p c g", g=2),
-                    op=ALU.subtract,
+                    out=t[("z", h)][:, mt, :, :].rearrange("p g c -> p (g c)"),
+                    in0=t[("q", h)][:, mt, :], in1=t[("lr", h)][:, mt, :], op=ALU.subtract,
                 )
 
         def var_out(h, mt=None):
@@ -501,8 +514,8 @@ def tile_chainlveg_pa_kernel(
                 nc.sync.dma_start(out=var_rows[:, :, cols(h, NH)], in_=t[("v", h)][:])
             else:
                 nc.vector.scalar_tensor_tensor(
-                    out=t[("v", h)][:, mt, :], in0=t[("lr", h)][:, mt, :], scalar=0.5,
-                    in1=t[("v", h)][:, mt, :], op0=ALU.mult, op1=ALU.add,
+                    out=pairs(t[("v", h)][:, mt, :]), in0=planes(t[("lr", h)][:, mt, :]), scalar=0.5,
+                    in1=pairs(t[("v", h)][:, mt, :]), op0=ALU.mult, op1=ALU.add,
                 )
                 nc.sync.dma_start(out=var_rows[:, mt, cols(h, NH)], in_=t[("v", h)][:, mt, :])
 
@@ -518,7 +531,7 @@ def tile_chainlveg_pa_kernel(
                     )
 
         def plane(a, mt, g):
-            return a[:, mt, :].rearrange("p (c g) -> p g c", g=2)[:, g, :]
+            return a[:, mt, g * (NH // 2) : (g + 1) * (NH // 2)]
 
         def pair_sum_terms(h, mt, kind, last):
             for g in range(2):

@@ -694,7 +694,8 @@ def tile_chainlveg_pa_kernel(
         for mt in range(MT):
             sum_z(1, mt)
             pair_sum_close(1, mt)
-        for h in range(H):
-            for mt in range(MT):
-                var_out(h, mt)
-                scale_out_scalar(h, mt)
+            var_out(0, mt)
+            scale_out_scalar(0, mt)
+        for mt in range(MT):
+            var_out(1, mt)
+            scale_out_scalar(1, mt)

@@ -298,6 +298,21 @@ def tile_chainlveg_pa_kernel(
                     )
                 acc[(h, mt, w)] = a
 
+        def matmuls_pass(h, w, c):
+            i = pieces.index((h, w, c))
+            for mt in range(MT):
+                if c == 0:
+                    acc[(h, mt, w)] = psum.tile([P, NH], F32, name="acc_%d_%d_%d" % (h, mt, w), tag="bank")
+                nc.tensor.matmul_mx(
+                    out=acc[(h, mt, w)][:],
+                    lhsT=xq[:, c, mt * P : (mt + 1) * P].bitcast(FP8X4),
+                    lhsT_scale=xs[:, c, mt * P : (mt + 1) * P],
+                    rhs=wq[:, i, :].bitcast(FP8X4),
+                    rhs_scale=ws[:, i, :],
+                    start=(c == 0),
+                    stop=(c == KP - 1),
+                )
+
         t = {}
         arow = {}
 
@@ -639,10 +654,11 @@ def tile_chainlveg_pa_kernel(
         evict(0, LSD, "v", 2)
         regroup(nc.vector.tensor_copy, M1, NH // 2, NH)
         quantise_w(W0)
+        matmuls_pass(1, LSD, 0)
         quantise_w(M0)
         clip_v(0)
         quantise_w(W1)
-        matmuls(1, LSD)
+        matmuls_pass(1, LSD, 1)
         quantise_w(M1)
         regroup_pool(W3, NH // 2)
         mean_clipped(0)

@@ -637,11 +637,12 @@ def tile_chainlveg_pa_kernel(
         keep_ie1e()
         quantise_w(V1)
         table_te_rest()
+        regroup_scalar(W0, 0)
         spread_bias()
         quantise_x(1)
         quantise_x(2)
         matmuls(0, LSD)
-        regroup_scalar(W0)
+        regroup_scalar(W0, 1)
         regroup_vector(M0)
         regroup_pool(M1, NH // 2)
         regroup_scalar(W1)

@@ -441,10 +441,12 @@ def tile_chainlveg_pa_kernel(
 
 
         def log_rho(h, scale):
-            nc.scalar.activation(
-                out=new("lr", h)[:].rearrange("p m (g c) -> p m c g", g=2),
-                in_=t[("rho", h)][:].rearrange("p m (c g) -> p m c g", g=2), func=ACT.Ln, scale=scale,
-            )
+            new("lr", h)
+            for mt in range(MT):
+                nc.scalar.activation(
+                    out=planes(t[("lr", h)][:, mt, :]), in_=pairs(t[("rho", h)][:, mt, :]), func=ACT.Ln,
+                    scale=scale,
+                )
 
         def cols(h, width):
             return slice(h * width, (h + 1) * width)

import math
from contextlib import ExitStack

import concourse.mybir as mybir
from concourse.masks import make_identity

F32 = mybir.dt.float32
BF16 = mybir.dt.bfloat16
U32 = mybir.dt.uint32
U8 = mybir.dt.uint8
I32 = mybir.dt.int32
FP8X4 = mybir.dt.float8_e4m3fn_x4
ALU = mybir.AluOpType
ACT = mybir.ActivationFunctionType

P = 128
MT = 3
K = 1024
KP = 2
N = 1024
NH = 512
H = 2
NI = 8
FLOPS = 2 * 384 * 1024 * 2048
MEAN = 0
LSD = 1
V_COLS = 336


def tile_chainlveg_pa_kernel(
    tc, x, s_weight, s_mu, s_var, tcm_w, tcm_b, tcv_w, tcv_b, out_0, out_1, out_2
):
    nc = tc.nc
    with ExitStack() as ctx:
        const = ctx.enter_context(tc.tile_pool(name="const", bufs=1))
        work = ctx.enter_context(tc.tile_pool(name="work", bufs=2))
        psum = ctx.enter_context(tc.psum_pool(name="psum", bufs=7))
        psum_keep = ctx.enter_context(tc.psum_pool(name="psum_keep", bufs=1))
        ctx.enter_context(tc.manual_schedule())

        x_rows = x.rearrange("b p d -> (b p) d").rearrange("(t q) d -> q t d", q=P)
        sm_rows = s_mu.rearrange("b p j e g -> (b p) (j e g)").rearrange("(t q) c -> q t c", q=P)
        sv_rows = s_var.rearrange("b p j e g -> (b p) (j e g)").rearrange("(t q) c -> q t c", q=P)
        sw_rows = s_weight.rearrange("b p j e -> (b p) (j e)").rearrange("(t q) c -> q t c", q=P)
        w_views = [w.rearrange("(c p j) n -> c p j n", c=KP, p=P, j=4) for w in (tcm_w, tcv_w)]
        sc_rows = out_0.rearrange("b p i j t e -> (b p) (i j t e)").rearrange("(t q) c -> q t c", q=P)
        mu_rows = out_1.rearrange("b p i j t e g -> (b p) (i j t e g)").rearrange("(t q) c -> q t c", q=P)
        var_rows = out_2.rearrange("b p i j t e g -> (b p) (i j t e g)").rearrange("(t q) c -> q t c", q=P)

        x_sb = const.tile([P, MT, K], BF16, name="x_sb")
        sv = const.tile([P, MT, 32], BF16, name="sv")
        sm = const.tile([P, MT, 32], BF16, name="sm")
        sw = const.tile([P, MT, 16], BF16, name="sw")
        btile = const.tile([P, P], BF16, name="btile")
        bcols = const.tile([P, 16], BF16, name="bcols")
        identb = const.tile([P, P], BF16, name="identb")
        ident = const.tile([P, P], F32, name="ident")
        onecol = const.tile([P, 1], F32, name="onecol")
        dummy = const.tile([P, 1], F32, name="dummy")
        neghalf = const.tile([P, P], F32, name="neghalf")
        poshalf = const.tile([P, P], F32, name="poshalf")
        te_rows = const.tile([P, MT, P], F32, name="te_rows")
        te_cols = const.tile([P, MT, P], F32, name="te_cols")
        sig_neg = const.tile([P, MT * 32], F32, name="sig_neg")
        sig_pos = const.tile([P, MT * 32], F32, name="sig_pos")
        inv_pos = const.tile([P, MT * 32], F32, name="inv_pos")
        v1e = const.tile([P, MT, 64], F32, name="v1e")
        m1e = const.tile([P, MT, 64], F32, name="m1e")
        m1m = const.tile([P, MT, 64], F32, name="m1m")
        m1m_rows = const.tile([P, MT, P], F32, name="m1m_rows")
        m1m_cols = const.tile([P, MT * P], F32, name="m1m_cols")
        twocol = const.tile([P, 1], F32, name="twocol")
        ie1e = const.tile([P, MT, 64], F32, name="ie1e")
        ie1_keep = psum_keep.tile([P, MT, 64], F32, name="ie1_keep")
        vsum = const.tile([P, MT * 16], F32, name="vsum")
        t0 = const.tile([P, MT * 16], F32, name="t0")
        xg = const.tile([P, MT, K], BF16, name="xg", align_bytes=64)
        xq = const.tile([P, KP, NH], U32, name="xq", align_bytes=64)
        xs = const.tile([P, KP, NH], U8, name="xs", align_bytes=64)
        bm1 = const.tile([P, 8], F32, name="bm1")
        wq = const.tile([P, 8, NH], U32, name="wq", align_bytes=64)
        ws = const.tile([P, 8, NH], U8, name="ws", align_bytes=64)
        bb = const.tile([P, N], BF16, name="bb")
        pieces = [(h, w, c) for h in range(H) for w in (LSD, MEAN) for c in range(KP)]
        raw = {}
        grouped = {}
        chain_of = {(0, MEAN, 1): "chain_a", (1, MEAN, 1): "chain_a"}
        for key in pieces:
            if key == (0, MEAN, 0):
                raw[key] = const.tile([P, 4, NH], BF16, name="raw_%d_%d_%d" % key, tag="chain_a", align_bytes=64)
            else:
                raw[key] = const.tile([P, 4, NH], BF16, name="raw_%d_%d_%d" % key)
            if key not in chain_of:
                grouped[key] = const.tile([P, NH, 4], BF16, name="grp_%d_%d_%d" % key, align_bytes=64)

        upper_half = const.tile([P, NH // 2, 4], BF16, name="upper_half", align_bytes=64)

        def regroup_pool(key, c1):
            grouped[key] = const.tile(
                [P, NH, 4], BF16, name="grp_%d_%d_%d" % key, tag=chain_of[key], align_bytes=64
            )
            nc.gpsimd.tensor_scalar(
                out=grouped[key][:, 0:c1, :],
                in0=raw[key][:, :, 0:c1].rearrange("p t c -> p c t"),
                scalar1=1.0, scalar2=0.0, op0=ALU.mult, op1=ALU.add,
            )

        def load_x(mt):
            nc.sync.dma_start(out=x_sb[:, mt, :], in_=x_rows[:, mt, :])

        def load_w(key):
            h, w, c = key
            nc.sync.dma_start(out=raw[key][:], in_=w_views[w][c, :, :, h * NH : (h + 1) * NH])

        def spread_t(ap):
            return (
                ap.rearrange("p (a g) -> p a g", g=2).unsqueeze(2).to_broadcast([P, MT * 16, 2, 2])
            )

        def as_jtg(a):
            return a[:].rearrange("p m (j t g) -> p (m j) t g", j=16, t=2, g=2)

        sm_flat = sm[:].rearrange("p m c -> p (m c)")
        sv_flat = sv[:].rearrange("p m c -> p (m c)")

        def table_v1():
            nc.vector.tensor_copy(out=as_jtg(v1e), in_=spread_t(sv_flat))

        def table_m1m():
            nc.vector.tensor_scalar(
                out=as_jtg(m1m), in0=spread_t(sm_flat), scalar1=-1.0, scalar2=None, op0=ALU.add
            )

        def table_m1m_rows():
            nc.vector.tensor_copy(
                out=m1m_rows[:].rearrange("p m (a c) -> p m a c", a=2),
                in_=m1m[:].unsqueeze(2).to_broadcast([P, MT, 2, 64]),
            )

        def table_m1e():
            nc.vector.tensor_copy(out=as_jtg(m1e), in_=spread_t(sm_flat))

        def m1m_turn():
            tp = psum.tile([P, MT * P], F32, name="tp_m1m", tag="bank")
            for mt in range(MT):
                nc.tensor.transpose(
                    out=tp[:, mt * P : (mt + 1) * P], in_=m1m_rows[:, mt, :], identity=ident[:]
                )
            nc.scalar.copy(out=m1m_cols[:], in_=tp[:])

        def table_inv_pos():
            nc.vector.reciprocal(out=inv_pos[:], in_=sig_pos[:])

        def table_ie1e():
            nc.vector.tensor_tensor(
                out=as_jtg(ie1e), in0=spread_t(sig_neg[:]), in1=spread_t(inv_pos[:]), op=ALU.mult
            )

        def keep_ie1e():
            nc.tensor.matmul(
                out=ie1_keep[:].rearrange("p m c -> p (m c)"), lhsT=ident[:],
                rhs=ie1e[:].rearrange("p m c -> p (m c)"), start=True, stop=True,
            )

        def table_vsum():
            sv_pairs = sv_flat.rearrange("p (a g) -> p a g", g=2)
            nc.vector.tensor_tensor(
                out=vsum[:], in0=sv_pairs[:, :, 0], in1=sv_pairs[:, :, 1], op=ALU.add
            )

        def table_t0():
            nc.vector.scalar_tensor_tensor(
                out=t0[:],
                in0=sw[:].rearrange("p m c -> p (m c)"),
                scalar=-math.log(2.0 * math.pi),
                in1=vsum[:],
                op0=ALU.add,
                op1=ALU.subtract,
            )

        def table_te_first():
            nc.vector.tensor_copy(
                out=te_rows[:, :, 0:32].rearrange("p m (j t) -> p m j t", t=2),
                in_=t0[:].rearrange("p (m j) -> p m j", m=MT).unsqueeze(3).to_broadcast([P, MT, 16, 2]),
            )

        def table_te_rest():
            nc.vector.tensor_copy(
                out=te_rows[:, :, 32:P].rearrange("p m (r c) -> p m r c", r=3),
                in_=te_rows[:, :, 0:32].unsqueeze(2).to_broadcast([P, MT, 3, 32]),
            )

        def te_turn():
            tp = psum.tile([P, MT, P], F32, name="tp", tag="bank")
            for mt in range(MT):
                nc.tensor.transpose(out=tp[:, mt, :], in_=te_rows[:, mt, :], identity=ident[:])
            nc.scalar.copy(out=te_cols[:], in_=tp[:])

        xw = x_sb[:].bitcast(F32)
        xg32 = xg[:].bitcast(F32)

        def x_turn(mt):
            xt = psum.tile([P, 4, P], F32, name="xt%d" % mt, tag="bank")
            for c in range(KP):
                for u in range(2):
                    nc.tensor.transpose(
                        out=xt[:, 2 * c + u, :],
                        in_=xw[:, mt, 256 * c + u : 256 * c + 256 : 2],
                        identity=ident[:],
                    )
            nc.scalar.copy(
                out=xg32[:, mt, :].rearrange("p (c r u) -> p c r u", c=KP, r=P, u=2),
                in_=xt[:].rearrange("p (c u) r -> p c r u", c=KP, u=2),
            )

        def quantise_x(mt):
            for c in range(KP):
                nc.vector.quantize_mx(
                    out=xq[:, c, mt * P : (mt + 1) * P].bitcast(FP8X4),
                    scales=xs[:, c, mt * P : (mt + 1) * P],
                    in_=xg[:, mt, c * 512 : (c + 1) * 512],
                )

        def regroup(copy, key, c0, c1):
            copy(
                out=grouped[key][:, c0:c1, :].rearrange("p (c i) t -> p c t i", i=4),
                in_=raw[key][:, :, c0:c1].rearrange("p t (c i) -> p c t i", i=4),
            )

        def regroup_both(key):
            regroup(nc.scalar.copy, key, V_COLS, NH)
            regroup(nc.vector.tensor_copy, key, 0, V_COLS)

        def regroup_vector(key):
            regroup(nc.vector.tensor_copy, key, 0, NH)

        def regroup_scalar(key, part=None):
            if part is None:
                regroup(nc.scalar.copy, key, 0, NH)
            else:
                regroup(nc.scalar.copy, key, part * (NH // 2), (part + 1) * (NH // 2))

        def quantise_w(key):
            i = pieces.index(key)
            nc.vector.quantize_mx(
                out=wq[:, i, :].bitcast(FP8X4),
                scales=ws[:, i, :],
                in_=grouped[key][:].rearrange("p w j -> p (w j)"),
            )

        def regroup_upper_scalar(key):
            nc.scalar.copy(
                out=upper_half[:].rearrange("p (c i) t -> p c t i", i=4),
                in_=raw[key][:, :, NH // 2 : NH].rearrange("p t (c i) -> p c t i", i=4),
            )

        def quantise_w_halves(key):
            i = pieces.index(key)
            for lo, src in ((0, grouped[key][:, 0 : NH // 2, :]), (NH // 2, upper_half[:])):
                nc.vector.quantize_mx(
                    out=wq[:, i, lo : lo + NH // 2].bitcast(FP8X4),
                    scales=ws[:, i, lo : lo + NH // 2],
                    in_=src.rearrange("p w j -> p (w j)"),
                )

        def bias_turn():
            btp = psum.tile([P, P], BF16, name="btp", tag="bank")
            nc.tensor.transpose(out=btp[:], in_=btile[:], identity=identb[:])
            nc.vector.tensor_copy(out=bcols[:], in_=btp[:, 0:16])
            nc.vector.tensor_scalar(
                out=bm1[:], in0=btp[:, 0:8], scalar1=1.0, scalar2=None, op0=ALU.add
            )

        def spread_bias():
            bp = psum.tile([P, 8, P], BF16, name="bp", tag="bank")
            for b in range(8):
                nc.tensor.transpose(
                    out=bp[:, b, :], in_=bcols[:, 8 + b : 9 + b].to_broadcast([P, P]),
                    identity=identb[:],
                )
            nc.scalar.copy(out=bb[:], in_=bp[:].rearrange("p b c -> p (b c)"))

        acc = {}

        def matmuls(h, w, only=None):
            for mt in range(MT) if only is None else (only,):
                a = psum.tile([P, NH], F32, name="acc_%d_%d_%d" % (h, mt, w), tag="bank")
                for c in range(KP):
                    i = pieces.index((h, w, c))
                    nc.tensor.matmul_mx(
                        out=a[:],
                        lhsT=xq[:, c, mt * P : (mt + 1) * P].bitcast(FP8X4),
                        lhsT_scale=xs[:, c, mt * P : (mt + 1) * P],
                        rhs=wq[:, i, :].bitcast(FP8X4),
                        rhs_scale=ws[:, i, :],
                        start=(c == 0),
                        stop=(c == KP - 1),
                    )
                acc[(h, mt, w)] = a

        def matmuls_pass(h, w, c):
            i = pieces.index((h, w, c))
            for mt in range(MT):
                if c == 0:
                    acc[(h, mt, w)] = psum.tile([P, NH], F32, name="acc_%d_%d_%d" % (h, mt, w), tag="bank")
                nc.tensor.matmul_mx(
                    out=acc[(h, mt, w)][:],
                    lhsT=xq[:, c, mt * P : (mt + 1) * P].bitcast(FP8X4),
                    lhsT_scale=xs[:, c, mt * P : (mt + 1) * P],
                    rhs=wq[:, i, :].bitcast(FP8X4),
                    rhs_scale=ws[:, i, :],
                    start=(c == 0),
                    stop=(c == KP - 1),
                )

        t = {}
        arow = {}

        def mean_products(h, nt):
            if nt == 0:
                t[("m", h)] = work.tile([P, 4, MT * P], F32, name="m_%d" % h, tag="m")
            at = psum.tile([P, NH], F32, name="at_%d_%d" % (h, nt), tag="bank")
            for c in range(KP):
                i = pieces.index((h, MEAN, c))
                nc.tensor.matmul_mx(
                    out=at[:],
                    lhsT=wq[:, i, nt * P : (nt + 1) * P].bitcast(FP8X4),
                    lhsT_scale=ws[:, i, nt * P : (nt + 1) * P],
                    rhs=xq[:, c, :].bitcast(FP8X4),
                    rhs_scale=xs[:, c, :],
                    start=(c == 0),
                    stop=(c == KP - 1),
                )
            nc.scalar.activation(
                out=t[("m", h)][:, nt, :], in_=at[:, 0 : MT * P], func=ACT.Relu,
                bias=bm1[:, h * 4 + nt : h * 4 + nt + 1], scale=1.0,
            )

        def mean_upper(h, nt):
            nc.scalar.activation(
                out=t[("m", h)][:, nt, :], in_=t[("m", h)][:, nt, :], func=ACT.Relu,
                bias=twocol[:, 0:1], scale=-1.0,
            )

        def mean_clipped(h):
            mean_products(h, 0)
            mean_products(h, 1)
            mean_upper(h, 0)
            mean_products(h, 2)
            mean_upper(h, 1)
            mean_products(h, 3)
            mean_upper(h, 2)
            mean_upper(h, 3)

        def mean_turn(h, nt):
            for mt in range(MT):
                if nt == 0:
                    arow[(h, mt)] = psum.tile([P, NH], F32, name="arow_%d_%d" % (h, mt), tag="bank")
                nc.tensor.matmul(
                    out=arow[(h, mt)][:, nt * P : (nt + 1) * P],
                    lhsT=t[("m", h)][:, nt, mt * P : (mt + 1) * P],
                    rhs=ident[:], is_transpose=True, start=True, stop=False,
                )
            for mt in range(MT):
                nc.tensor.matmul(
                    out=arow[(h, mt)][:, nt * P : (nt + 1) * P],
                    lhsT=m1m_cols[:, mt * P : (mt + 1) * P],
                    rhs=ident[:], is_transpose=True, start=False, stop=True,
                )

        def mean_front(h):
            mean_products(h, 0)
            mean_products(h, 1)
            mean_turn(h, 0)
            mean_turn(h, 1)
            mean_products(h, 2)
            mean_products(h, 3)
            mean_turn(h, 2)
            mean_turn(h, 3)

        def new(kind, h, cols=NH):
            a = work.tile([P, MT, cols], F32, name="%s_%d" % (kind, h), tag=kind)
            t[(kind, h)] = a
            return a

        def all_i(tab, cols):
            return tab[:].unsqueeze(2).to_broadcast([P, MT, NI, cols])

        def one_i(tab, mt, cols):
            return tab[:, mt, :].unsqueeze(1).to_broadcast([P, NI, cols])

        def by_i(a):
            return a[:].rearrange("p m (i c) -> p m i c", i=NI)

        def by_i1(a, mt):
            return a[:, mt, :].rearrange("p (i c) -> p i c", i=NI)

        def pairs(ap):
            return ap.rearrange("p (c g) -> p c g", g=2)

        def planes(ap):
            return ap.rearrange("p (g c) -> p c g", g=2)

        def by_gi(a, mt):
            return a[:, mt, :].rearrange("p (g i c) -> p g i c", g=2, i=NI)

        def table_gi(tab, mt):
            return (
                tab[:, mt, :].rearrange("p (c g) -> p g c", g=2).unsqueeze(2).to_broadcast([P, 2, NI, 32])
            )

        def flat(a):
            return a[:].rearrange("p m c -> p (m c)")

        def evict(h, w, kind, mt):
            if mt == 0:
                new(kind, h)
            nc.vector.tensor_tensor(
                out=t[(kind, h)][:, mt, :], in0=acc[(h, mt, w)][:],
                in1=bb[:, h * NH : (h + 1) * NH], op=ALU.add,
            )

        def clip_v(h):
            nc.vector.tensor_scalar(
                out=flat(t[("v", h)]), in0=flat(t[("v", h)]), scalar1=1.0, scalar2=-1.0,
                op0=ALU.min, op1=ALU.max,
            )

        def diff_v(h):
            nc.vector.tensor_tensor(
                out=by_i(new("rho", h)), in0=by_i(t[("v", h)]), in1=all_i(v1e, 64), op=ALU.subtract
            )

        def load_sigmoid_table():
            nc.scalar.activation(out=dummy[:], in_=onecol[:], func=ACT.Sigmoid)

        def sigmoid(h, scale):
            nc.scalar.activation(
                out=flat(t[("rho", h)]), in_=flat(t[("rho", h)]), func=ACT.Sigmoid, scale=scale
            )


        def log_rho(h, scale):
            new("lr", h)
            for mt in range(MT):
                nc.scalar.activation(
                    out=planes(t[("lr", h)][:, mt, :]), in_=pairs(t[("rho", h)][:, mt, :]), func=ACT.Ln,
                    scale=scale,
                )

        def cols(h, width):
            return slice(h * width, (h + 1) * width)

        def prod_a(h):
            new("a", h)
            for mt in range(MT):
                nc.vector.tensor_tensor(
                    out=t[("a", h)][:, mt, :], in0=arow[(h, mt)][:], in1=t[("rho", h)][:, mt, :],
                    op=ALU.mult,
                )

        def prod_q1(h):
            new("q", h)
            for mt in range(MT):
                nc.vector.tensor_tensor(
                    out=planes(t[("q", h)][:, mt, :]), in0=pairs(arow[(h, mt)][:]),
                    in1=pairs(t[("a", h)][:, mt, :]), op=ALU.mult,
                )

        def mean_out(h, mt=None):
            if mt is None:
                nc.vector.tensor_tensor(
                    out=by_i(t[("a", h)]), in0=all_i(m1e, 64), in1=by_i(t[("a", h)]), op=ALU.subtract
                )
                nc.sync.dma_start(out=mu_rows[:, :, cols(h, NH)], in_=t[("a", h)][:])
            else:
                nc.vector.tensor_tensor(
                    out=by_i1(t[("a", h)], mt), in0=one_i(m1e, mt, 64), in1=by_i1(t[("a", h)], mt),
                    op=ALU.subtract,
                )
                nc.sync.dma_start(out=mu_rows[:, mt, cols(h, NH)], in_=t[("a", h)][:, mt, :])

        def mean_out_pool(h, mt):
            if mt == 0:
                new("mu", h)
            nc.gpsimd.tensor_tensor(
                out=by_i1(t[("mu", h)], mt), in0=one_i(m1e, mt, 64), in1=by_i1(t[("a", h)], mt),
                op=ALU.subtract,
            )
            nc.sync.dma_start(out=mu_rows[:, mt, cols(h, NH)], in_=t[("mu", h)][:, mt, :])

        def prod_q2_pool(h, mt):
            nc.gpsimd.tensor_tensor(
                out=by_gi(t[("q", h)], mt), in0=by_gi(t[("q", h)], mt), in1=table_gi(ie1e, mt),
                op=ALU.mult,
            )

        def prod_q2(h, mt=None):
            if mt is None:
                nc.vector.tensor_tensor(
                    out=by_i(t[("q", h)]), in0=by_i(t[("q", h)]), in1=all_i(ie1_keep, 64), op=ALU.mult
                )
            else:
                nc.vector.tensor_tensor(
                    out=by_gi(t[("q", h)], mt), in0=by_gi(t[("q", h)], mt), in1=table_gi(ie1_keep, mt),
                    op=ALU.mult,
                )

        def sum_z(h, mt=None):
            if mt is None or mt == 0:
                t[("z", h)] = work.tile([P, MT, 2, NH // 2], F32, name="z_%d" % h, tag="d")
            if mt is None:
                nc.vector.tensor_tensor(
                    out=t[("z", h)][:].rearrange("p m g c -> p m c g"),
                    in0=t[("q", h)][:].rearrange("p m (c g) -> p m c g", g=2),
                    in1=t[("lr", h)][:].rearrange("p m (c g) -> p m c g", g=2),
                    op=ALU.subtract,
                )
            else:
                nc.vector.tensor_tensor(
                    out=t[("z", h)][:, mt, :, :].rearrange("p g c -> p (g c)"),
                    in0=t[("q", h)][:, mt, :], in1=t[("lr", h)][:, mt, :], op=ALU.subtract,
                )

        def var_out(h, mt=None):
            if mt is None:
                nc.vector.scalar_tensor_tensor(
                    out=flat(t[("v", h)]), in0=flat(t[("lr", h)]), scalar=0.5,
                    in1=flat(t[("v", h)]), op0=ALU.mult, op1=ALU.add,
                )
                nc.sync.dma_start(out=var_rows[:, :, cols(h, NH)], in_=t[("v", h)][:])
            else:
                nc.vector.scalar_tensor_tensor(
                    out=pairs(t[("v", h)][:, mt, :]), in0=planes(t[("lr", h)][:, mt, :]), scalar=0.5,
                    in1=pairs(t[("v", h)][:, mt, :]), op0=ALU.mult, op1=ALU.add,
                )
                nc.sync.dma_start(out=var_rows[:, mt, cols(h, NH)], in_=t[("v", h)][:, mt, :])

        zps = {}

        def pair_sum_open(h):
            for mt in range(MT):
                zps[(h, mt)] = psum.tile([P, NH // 2], F32, name="zp_%d_%d" % (h, mt), tag="bank")
                for b in range(2):
                    nc.tensor.matmul(
                        out=zps[(h, mt)][:, b * P : (b + 1) * P], lhsT=te_cols[:, mt, :], rhs=ident[:],
                        is_transpose=True, start=(b == 0), stop=False,
                    )

        def plane(a, mt, g):
            return a[:, mt, g * (NH // 2) : (g + 1) * (NH // 2)]

        def pair_sum_terms(h, mt, kind, last):
            for g in range(2):
                nc.tensor.matmul(
                    out=zps[(h, mt)][:], lhsT=(neghalf if kind == "q" else poshalf)[:],
                    rhs=plane(t[(kind, h)], mt, g), start=False, stop=(last and g == 1),
                )

        def pair_sum_close(h, mt):
            nc.tensor.matmul(
                out=zps[(h, mt)][:], lhsT=neghalf[:], rhs=t[("z", h)][:, mt, 0, :],
                start=False, stop=False,
            )
            nc.tensor.matmul(
                out=zps[(h, mt)][:], lhsT=neghalf[:], rhs=t[("z", h)][:, mt, 1, :],
                start=False, stop=True,
            )

        def scale_out_scalar(h, mt):
            if mt == 0:
                new("sc", h, NH // 2)
            nc.scalar.copy(out=t[("sc", h)][:, mt, :], in_=zps[(h, mt)][:])
            queue = (nc.scalar, nc.sync)[h]
            queue.dma_start(out=sc_rows[:, mt, cols(h, NH // 2)], in_=t[("sc", h)][:, mt, :])

        def pair_sum_vector(h):
            nc.vector.tensor_tensor(
                out=new("zs", h, NH // 2)[:], in0=t[("z", h)][:, :, 0, :], in1=t[("z", h)][:, :, 1, :],
                op=ALU.add,
            )

        def scale_out_vector(h, shift):
            a = new("sc", h, NH // 2)
            for mt in range(MT):
                nc.vector.scalar_tensor_tensor(
                    out=by_i1(a, mt), in0=by_i1(t[("zs", h)], mt), scalar=-0.5,
                    in1=te_rows[:, mt, shift : shift + 32].unsqueeze(1).to_broadcast([P, NI, 32]),
                    op0=ALU.mult, op1=ALU.add,
                )
                nc.sync.dma_start(out=sc_rows[:, mt, cols(h, NH // 2)], in_=a[:, mt, :])

        V0, V1, M0, M1 = (0, LSD, 0), (0, LSD, 1), (0, MEAN, 0), (0, MEAN, 1)
        W0, W1, W2, W3 = (1, LSD, 0), (1, LSD, 1), (1, MEAN, 0), (1, MEAN, 1)
        nc.gpsimd.memset(onecol[:], 1.0)
        nc.scalar.dma_start(out=sv[:], in_=sv_rows)
        nc.scalar.dma_start(out=sm[:], in_=sm_rows)
        nc.scalar.dma_start(out=sw[:], in_=sw_rows)
        nc.gpsimd.memset(btile[:], 0.0)
        nc.scalar.dma_start(out=btile[0:8, :], in_=tcm_b.rearrange("(r c) -> r c", c=P))
        nc.scalar.dma_start(out=btile[8:16, :], in_=tcv_b.rearrange("(r c) -> r c", c=P))
        load_sigmoid_table()
        load_w(V0)
        load_x(0)
        load_w(V1)
        load_x(1)
        load_x(2)
        for key in (W0, M0, M1, W1, W2, W3):
            load_w(key)
        make_identity(nc, identb[:])
        make_identity(nc, ident[:])
        nc.gpsimd.memset(twocol[:], 2.0)
        for sign, half_ident in ((-0.5, neghalf), (0.5, poshalf)):
            nc.gpsimd.tensor_scalar(
                out=half_ident[:], in0=ident[:], scalar1=sign, scalar2=0.0, op0=ALU.mult, op1=ALU.add
            )
        nc.scalar.activation(out=sig_pos[:], in_=sv_flat, func=ACT.Sigmoid, scale=2.0)
        nc.scalar.activation(out=sig_neg[:], in_=sv_flat, func=ACT.Sigmoid, scale=-2.0)

        nc.vector.memset(xq[:, :, MT * P : NH].bitcast(I32), 0)
        nc.vector.memset(xs[:, :, MT * P : NH].bitcast(I32), 0)
        table_v1()
        table_inv_pos()
        regroup_both(V0)
        x_turn(0)
        table_m1m()
        table_m1e()
        table_ie1e()
        table_vsum()
        table_m1m_rows()
        regroup_both(V1)
        x_turn(1)
        quantise_x(0)
        table_t0()
        x_turn(2)
        quantise_w(V0)
        table_te_first()
        bias_turn()
        keep_ie1e()
        quantise_w(V1)
        table_te_rest()
        regroup_scalar(W0, 0)
        spread_bias()
        quantise_x(1)
        quantise_x(2)
        matmuls(0, LSD)
        regroup_scalar(W0, 1)
        regroup_vector(M0)
        regroup_pool(M1, NH // 2)
        regroup_scalar(W1)
        m1m_turn()
        te_turn()
        regroup_scalar(W2)
        regroup_upper_scalar(W3)
        evict(0, LSD, "v", 0)
        evict(0, LSD, "v", 1)
        evict(0, LSD, "v", 2)
        regroup(nc.vector.tensor_copy, M1, NH // 2, NH)
        quantise_w(W0)
        matmuls_pass(1, LSD, 0)
        quantise_w(M0)
        clip_v(0)
        quantise_w(W1)
        matmuls_pass(1, LSD, 1)
        quantise_w(M1)
        regroup_pool(W3, NH // 2)
        mean_clipped(0)
        evict(1, LSD, "v", 0)
        evict(1, LSD, "v", 1)
        evict(1, LSD, "v", 2)
        diff_v(0)
        sigmoid(0, -2.0)
        quantise_w(W2)
        mean_turn(0, 0)
        mean_turn(0, 1)
        quantise_w_halves(W3)
        mean_products(1, 0)
        mean_products(1, 1)
        mean_turn(0, 2)
        mean_turn(0, 3)
        clip_v(1)
        mean_upper(1, 0)
        mean_products(1, 2)
        mean_upper(1, 1)
        mean_products(1, 3)
        mean_upper(1, 2)
        mean_upper(1, 3)
        diff_v(1)
        sigmoid(1, -2.0)
        log_rho(0, 1.0)
        log_rho(1, 1.0)
        prod_a(0)
        for mt in range(MT):
            mean_out_pool(0, mt)
        prod_q1(0)
        for nt in range(4):
            mean_turn(1, nt)
        pair_sum_open(0)
        prod_q2_pool(0, 2)
        for mt in range(MT - 1):
            prod_q2(0, mt)
            pair_sum_terms(0, mt, "q", False)
        pair_sum_terms(0, 2, "q", False)
        prod_a(1)
        for mt in range(MT):
            mean_out_pool(1, mt)
        prod_q1(1)
        pair_sum_open(1)
        for mt in range(MT):
            prod_q2(1, mt)
        for mt in range(MT):
            pair_sum_terms(0, mt, "lr", True)
        for mt in range(MT):
            sum_z(1, mt)
            pair_sum_close(1, mt)
            var_out(0, mt)
            scale_out_scalar(0, mt)
        for mt in range(MT):
            var_out(1, mt)
            scale_out_scalar(1, mt)
